import numpy as np
import ml_dtypes


def mxq(x, axis, fmt="e4m3"):
    dtype, down = {"e4m3": (ml_dtypes.float8_e4m3fn, 7), "e5m2": (ml_dtypes.float8_e5m2, 14)}[fmt]
    v = np.moveaxis(np.asarray(x, np.float32).astype(ml_dtypes.bfloat16).astype(np.float64), axis, -1)
    blocks = v.reshape(v.shape[:-1] + (-1, 32))
    amax = np.abs(blocks).max(-1, keepdims=True)
    byte = np.maximum(np.where(amax > 0, np.frexp(amax)[1] - 1 + 127, 0) - down, 1)
    scale = np.exp2(byte - 127.0)
    codes = (blocks / scale).astype(np.float32).astype(dtype).astype(np.float64)
    return np.moveaxis((codes * scale).reshape(v.shape), -1, axis)


WIDE = False


def mx_kscale(k):
    if not WIDE:
        return np.ones(k)
    levels = np.array([10, -10, 5, -5, 0])
    a = np.random.permutation(np.resize(levels, k // 512 * 4)).reshape(k // 512, 4)
    idx = np.arange(k)
    return np.exp2(a[idx // 512, idx % 128 // 32])


BF16 = ml_dtypes.bfloat16


def bf(x):
    return np.asarray(x, np.float32).astype(BF16)


def f64(x):
    return np.asarray(x).astype(np.float64)


E2M1 = np.array([0.0, 0.5, 1.0, 1.5, 2.0, 3.0, 4.0, 6.0, -0.0, -0.5, -1.0, -1.5, -2.0, -3.0, -4.0, -6.0])


def pack_weight(w, fmt):
    k, n = w.shape
    w = f64(bf(w)).reshape(k // 32, 32, n)
    amax = np.abs(w).max(1)
    if fmt == "e4m3":
        byte = np.frexp(amax)[1] - 1 + 127 - 7
    else:
        mant, ex = np.frexp(amax / 6.0)
        byte = np.where(mant > 0.5, ex, ex - 1) + 127
    byte = np.clip(np.where(amax > 0, byte, 1), 1, 254)
    scaled = (w * np.exp2(127.0 - byte)[:, None, :]).reshape(k, n).astype(np.float32)
    by_word = np.ascontiguousarray(scaled.reshape(k // 512, 128, 4, n).transpose(0, 1, 3, 2))
    if fmt == "e4m3":
        words = by_word.astype(ml_dtypes.float8_e4m3fn).view(np.uint8)
    else:
        c = by_word.astype(ml_dtypes.float4_e2m1fn).view(np.uint8) & 0xF
        words = c[..., 0::2] | (c[..., 1::2] << 4)
    return np.ascontiguousarray(words), np.ascontiguousarray(byte.astype(np.uint8).reshape(k // 512, 16, n))


def unpack_weight(words, scales, fmt):
    g, p, n, _ = words.shape
    if fmt == "e4m3":
        vals = np.ascontiguousarray(words).view(ml_dtypes.float8_e4m3fn).astype(np.float64)
    else:
        nib = np.empty((g, p, n, 4), np.uint8)
        nib[..., 0::2] = words & 0xF
        nib[..., 1::2] = words >> 4
        vals = E2M1[nib]
    vals = vals * np.repeat(np.exp2(scales.astype(np.float64) - 127.0), 8, axis=1)[..., None]
    return vals.transpose(0, 1, 3, 2).reshape(g * 512, n)


B, SI, ST, DM, H, D = 4, 1536, 512, 1024, 1, 128
S = ST + SI
HD = H * D
EPS = 1e-6
FMT = "e4m3"


def rms_norm(x, gamma):
    var = np.mean(x * x, axis=-1, keepdims=True)
    return x * (1.0 / np.sqrt(var + EPS)) * gamma


def apply_rotary(x, cos, sin):
    xr = x.reshape(B, S, H, D // 2, 2)
    x1, x2 = xr[..., 0], xr[..., 1]
    rot = np.stack([-x2, x1], axis=-1).reshape(B, S, H, D)
    return x * cos[None, :, None, :] + rot * sin[None, :, None, :]


def heads(y):
    return y.reshape(B, -1, H, D)


def setup_inputs():
    s = mx_kscale(DM)
    w = 1.0 / np.sqrt(DM)
    pos = np.arange(S)[:, None]
    inv = 1.0 / (10000.0 ** (np.arange(0, D, 2) / D))
    ang = np.repeat(pos * inv[None, :], 2, axis=-1)
    inp = {"hidden_states": bf(np.random.standard_normal((B, SI, DM)) * s),
           "encoder_hidden_states": bf(np.random.standard_normal((B, ST, DM)) * s),
           "rope_cos": bf(np.cos(ang)), "rope_sin": bf(np.sin(ang))}
    for n in ["Wq", "Wk", "Waq", "Wak"]:
        words, scales = pack_weight(np.random.standard_normal((DM, HD)) * w / s[:, None], FMT)
        inp[n + "_words"] = words
        inp[n + "_scales"] = scales
    for n in ["bq", "bk", "baq", "bak"]:
        inp[n] = bf(np.random.standard_normal(HD) * 0.3)
    for n in ["g_q", "g_k", "g_aq", "g_ak"]:
        inp[n] = bf(1.5 * (1.0 + 0.1 * np.random.standard_normal(D)))
    return inp


def reference(hidden_states, encoder_hidden_states, rope_cos, rope_sin, Wq_words, Wq_scales, bq, Wk_words, Wk_scales, bk, Waq_words, Waq_scales, baq, Wak_words, Wak_scales, bak, g_q, g_k, g_aq, g_ak):
    xq = mxq(f64(hidden_states), 2, "e4m3")
    cq = mxq(f64(encoder_hidden_states), 2, "e4m3")
    q = rms_norm(heads((xq @ unpack_weight(Wq_words, Wq_scales, FMT)) + f64(bq)), f64(g_q))
    k = rms_norm(heads((xq @ unpack_weight(Wk_words, Wk_scales, FMT)) + f64(bk)), f64(g_k))
    eq = rms_norm(heads((cq @ unpack_weight(Waq_words, Waq_scales, FMT)) + f64(baq)), f64(g_aq))
    ek = rms_norm(heads((cq @ unpack_weight(Wak_words, Wak_scales, FMT)) + f64(bak)), f64(g_ak))
    q = np.concatenate([eq, q], axis=1)
    k = np.concatenate([ek, k], axis=1)
    return apply_rotary(q, f64(rope_cos), f64(rope_sin)), apply_rotary(k, f64(rope_cos), f64(rope_sin))

@@ -1,0 +1,286 @@
+from contextlib import ExitStack
+
+import concourse.mybir as mybir
+from concourse.masks import make_identity
+
+F32 = mybir.dt.float32
+BF16 = mybir.dt.bfloat16
+I32 = mybir.dt.int32
+U32 = mybir.dt.uint32
+U8 = mybir.dt.uint8
+FP8X4 = mybir.dt.float8_e4m3fn_x4
+ACT = mybir.ActivationFunctionType
+ALU = mybir.AluOpType
+
+P = 128
+BATCH = 4
+TEXT_ROWS = 512
+SEQ = 2048
+K = 1024
+D = 128
+HALF = D // 2
+EPS = 1e-6
+
+K_PASS = 4 * P
+PASSES = K // K_PASS
+PASS_WORDS = K_PASS // 2
+ROWS_PER_PART = 4
+CHUNK = P * ROWS_PER_PART
+SEQ_CHUNKS = SEQ // CHUNK
+N_CHUNKS = BATCH * SEQ_CHUNKS
+LOAD_AHEAD = 3
+
+FLOPS = 2 * BATCH * SEQ * K * 2 * D
+
+
+def tile_fluxjointattention_pa_t_kernel(
+    tc,
+    hidden_states,
+    encoder_hidden_states,
+    rope_cos,
+    rope_sin,
+    Wq_words,
+    Wq_scales,
+    Wk_words,
+    Wk_scales,
+    Waq_words,
+    Waq_scales,
+    Wak_words,
+    Wak_scales,
+    bq,
+    bk,
+    baq,
+    bak,
+    g_q,
+    g_k,
+    g_aq,
+    g_ak,
+    out_0,
+    out_1,
+):
+    nc = tc.nc
+    weights = [(Wq_words, Wq_scales), (Wk_words, Wk_scales), (Waq_words, Waq_scales), (Wak_words, Wak_scales)]
+    biases = [bq, bk, baq, bak]
+    gains = [g_q, g_k, g_aq, g_ak]
+    outs = [out_0, out_1]
+
+    def first_weight(s):
+        return 2 if s == 0 else 0
+
+    with ExitStack() as ctx:
+        const = ctx.enter_context(tc.tile_pool(name="const", bufs=1))
+        x_pool = ctx.enter_context(tc.tile_pool(name="x", bufs=LOAD_AHEAD + 1))
+        work = ctx.enter_context(tc.tile_pool(name="work", bufs=2))
+        out_pool = ctx.enter_context(tc.tile_pool(name="out", bufs=3))
+        turned_pool = ctx.enter_context(tc.psum_pool(name="turned", bufs=4))
+        acc_pool = ctx.enter_context(tc.psum_pool(name="acc", bufs=2))
+        back_pool = ctx.enter_context(tc.psum_pool(name="back", bufs=2))
+
+        def load(c):
+            s, b = divmod(c, BATCH)
+            if s == 0:
+                rows = encoder_hidden_states[b]
+            else:
+                rows = hidden_states[b, (s - 1) * CHUNK : s * CHUNK, :]
+            x_rows = x_pool.tile([P, ROWS_PER_PART, K], BF16)
+            nc.sync.dma_start(out=x_rows[:], in_=rows.rearrange("(p t) k -> p t k", t=ROWS_PER_PART))
+            return x_rows
+
+        x_tiles = {}
+        x_tiles[0] = load(0)
+
+        eps = const.tile([P, 1], F32)
+        nc.vector.memset(eps[:], EPS)
+        warm = const.tile([P, 1], F32)
+        nc.scalar.activation(out=warm[:], in_=eps[:], func=ACT.Sqrt)
+
+        ident = const.tile([P, P], F32)
+        make_identity(nc, ident[:])
+        even_first = const.tile([P, P], F32)
+        nc.vector.tensor_copy(
+            out=even_first[:].rearrange("p (e i) -> p e i", e=2),
+            in_=ident[:].rearrange("p (i e) -> p e i", e=2),
+        )
+
+        w_words = const.tile([P, 4, PASSES, D], U32, align_bytes=64)
+        w_scales = const.tile([P, 4, PASSES, D], U8, align_bytes=64)
+        nc.vector.memset(w_scales[:].bitcast(I32), 0)
+        for w in (2, 3, 0, 1):
+            words, scales = weights[w]
+            nc.sync.dma_start(
+                out=w_words[:, w].bitcast(I32),
+                in_=words.rearrange("g p n t -> p g (n t)").bitcast(I32),
+            )
+            scale_rows = scales.rearrange("g (q r) n -> q r g n", r=4)
+            for q in range(4):
+                nc.sync.dma_start(
+                    out=w_scales[32 * q : 32 * q + 4, w].bitcast(I32),
+                    in_=scale_rows[q].bitcast(I32),
+                )
+
+        bias_rows = const.tile([P, P], BF16)
+        nc.vector.memset(bias_rows[:], 0.0)
+        for w in range(4):
+            nc.scalar.dma_start(out=bias_rows[w : w + 1, :], in_=biases[w].rearrange("(o d) -> o d", o=1))
+        bias_rows32 = const.tile([P, P], F32)
+        nc.vector.tensor_copy(out=bias_rows32[:], in_=bias_rows[:])
+        bias_turned = turned_pool.tile([P, 2, 2 * P], F32, tag="turned")
+        nc.tensor.transpose(out=bias_turned[:, 0, 0:P], in_=bias_rows32[:], identity=ident[:])
+        bias_col = const.tile([P, 4], F32)
+        nc.vector.tensor_copy(out=bias_col[:], in_=bias_turned[:, 0, 0:4])
+
+        gain_row = const.tile([P, 4 * D], BF16)
+        nc.vector.memset(gain_row[:], 0.0)
+        for w in range(4):
+            nc.scalar.dma_start(
+                out=gain_row[0:1, w * D : (w + 1) * D], in_=gains[w].rearrange("(o d) -> o d", o=1)
+            )
+        ones = const.tile([P, P], BF16)
+        nc.vector.memset(ones[:], 1.0)
+        gain_all = acc_pool.tile([P, 4 * D], F32, tag="acc")
+        nc.tensor.matmul(out=gain_all[:], lhsT=ones[:], rhs=gain_row[:], start=True, stop=True)
+        gain_pairs = gain_all[:].rearrange("p (w i e) -> p w e i", w=4, e=2)
+        gain_c = const.tile([P, 4, D], F32)
+        nc.vector.tensor_copy(out=gain_c[:].rearrange("p w (e i) -> p w e i", e=2), in_=gain_pairs)
+        gain_s = const.tile([P, 4, D], F32)
+        nc.vector.tensor_scalar_mul(out=gain_s[:, :, 0:HALF], in0=gain_pairs[:, :, 1, :], scalar1=-1.0)
+        nc.vector.tensor_copy(out=gain_s[:, :, HALF:D], in_=gain_pairs[:, :, 0, :])
+
+        cos_rows = const.tile([P, SEQ_CHUNKS, ROWS_PER_PART, D], BF16)
+        sin_rows = const.tile([P, SEQ_CHUNKS, ROWS_PER_PART, D], BF16)
+        for rows, table in ((cos_rows, rope_cos), (sin_rows, rope_sin)):
+            nc.scalar.dma_start(
+                out=rows[:].rearrange("p s t d -> p s (t d)"),
+                in_=table.rearrange("(s p t) d -> p s (t d)", s=SEQ_CHUNKS, t=ROWS_PER_PART),
+            )
+
+        for c in range(1, LOAD_AHEAD):
+            x_tiles[c] = load(c)
+
+        table_c = const.tile([P, SEQ_CHUNKS, 2, ROWS_PER_PART, D], F32)
+        table_s = const.tile([P, SEQ_CHUNKS, 2, ROWS_PER_PART, D], F32)
+        for s in range(SEQ_CHUNKS):
+            for h in range(2):
+                w = first_weight(s) + h
+                for table, rows, gain in ((table_c, cos_rows, gain_c), (table_s, sin_rows, gain_s)):
+                    nc.gpsimd.tensor_tensor(
+                        out=table[:, s, h].rearrange("p t (e i) -> p t e i", e=2),
+                        in0=rows[:, s].rearrange("p t (i e) -> p t e i", e=2),
+                        in1=gain[:, w]
+                        .rearrange("p (e i) -> p e i", e=2)
+                        .unsqueeze(1)
+                        .to_broadcast([P, ROWS_PER_PART, 2, HALF]),
+                        op=ALU.mult,
+                    )
+
+        squares = const.tile([P, D], F32)
+
+        def turn_and_quantise(x_rows):
+            x_words = x_rows[:].bitcast(F32)
+            grouped = work.tile([P, PASSES, 4 * CHUNK], BF16, align_bytes=64)
+            codes = work.tile([P, PASSES, CHUNK], U32, align_bytes=64)
+            scales = work.tile([P, PASSES, CHUNK], U8, align_bytes=64)
+            for g in range(PASSES):
+                grouped_words = grouped[:, g, :].bitcast(F32).rearrange("p (n u) -> p n u", u=2)
+                for half in range(2):
+                    turned = turned_pool.tile([P, 2, 2 * P], F32, tag="turned")
+                    for j in range(2):
+                        t = 2 * half + j
+                        for u in range(2):
+                            nc.tensor.transpose(
+                                out=turned[:, u, j * P : (j + 1) * P],
+                                in_=x_words[:, t, PASS_WORDS * g + u : PASS_WORDS * (g + 1) : 2],
+                                identity=ident[:],
+                            )
+                    nc.scalar.copy(
+                        out=grouped_words[:, 2 * P * half : 2 * P * (half + 1), :],
+                        in_=turned[:].rearrange("p u n -> p n u"),
+                    )
+                nc.vector.quantize_mx(
+                    out=codes[:, g, :].bitcast(FP8X4), scales=scales[:, g, :], in_=grouped[:, g, :]
+                )
+            return codes, scales
+
+        def project(s, codes, scales):
+            y_cols = work.tile([P, 2, CHUNK], F32)
+            for h in range(2):
+                w = first_weight(s) + h
+                acc = acc_pool.tile([P, CHUNK], F32, tag="acc")
+                for g in range(PASSES):
+                    nc.tensor.matmul_mx(
+                        out=acc[:],
+                        lhsT=w_words[:, w, g, :].bitcast(FP8X4),
+                        lhsT_scale=w_scales[:, w, g, :],
+                        rhs=codes[:, g, :].bitcast(FP8X4),
+                        rhs_scale=scales[:, g, :],
+                        start=(g == 0),
+                        stop=(g == PASSES - 1),
+                    )
+                nc.scalar.activation(
+                    out=y_cols[:, h, :], in_=acc[:], func=ACT.Identity, bias=bias_col[:, w : w + 1], scale=1.0
+                )
+            return y_cols
+
+        def norm_rotate_store(s, b, y_cols):
+            sum_sq = work.tile([P, 2, ROWS_PER_PART], F32)
+            rms = work.tile([P, 2, ROWS_PER_PART], F32)
+            inv_rms = work.tile([P, 2, ROWS_PER_PART], F32)
+            own = work.tile([P, 2, ROWS_PER_PART, D], F32)
+            partner = work.tile([P, 2, ROWS_PER_PART, D], F32)
+            result = out_pool.tile([P, 2, ROWS_PER_PART, D], F32)
+            for h in range(2):
+                y = back_pool.tile([P, ROWS_PER_PART, D], F32)
+                for t in range(ROWS_PER_PART):
+                    nc.tensor.transpose(
+                        out=y[:, t, :], in_=y_cols[:, h, t * P : (t + 1) * P], identity=even_first[:]
+                    )
+                for t in range(ROWS_PER_PART):
+                    nc.scalar.activation(
+                        out=squares[:], in_=y[:, t, :], func=ACT.Square, accum_out=sum_sq[:, h, t : t + 1]
+                    )
+                nc.scalar.activation(
+                    out=rms[:, h, :], in_=sum_sq[:, h, :], func=ACT.Sqrt, bias=eps[:, 0:1], scale=1.0 / D
+                )
+                nc.vector.reciprocal(out=inv_rms[:, h, :], in_=rms[:, h, :])
+                for t in range(ROWS_PER_PART):
+                    r = inv_rms[:, h, t : t + 1]
+                    nc.vector.scalar_tensor_tensor(
+                        out=own[:, h, t, :], in0=y[:, t, :], scalar=r, in1=table_c[:, s, h, t, :],
+                        op0=ALU.mult, op1=ALU.mult,
+                    )
+                    nc.vector.scalar_tensor_tensor(
+                        out=partner[:, h, t, 0:HALF], in0=y[:, t, HALF:D], scalar=r,
+                        in1=table_s[:, s, h, t, 0:HALF], op0=ALU.mult, op1=ALU.mult,
+                    )
+                    nc.vector.scalar_tensor_tensor(
+                        out=partner[:, h, t, HALF:D], in0=y[:, t, 0:HALF], scalar=r,
+                        in1=table_s[:, s, h, t, HALF:D], op0=ALU.mult, op1=ALU.mult,
+                    )
+            for h in range(2):
+                nc.vector.tensor_tensor(
+                    out=result[:, h].rearrange("p t (i e) -> p t i e", e=2),
+                    in0=own[:, h].rearrange("p t (e i) -> p t i e", e=2),
+                    in1=partner[:, h].rearrange("p t (e i) -> p t i e", e=2),
+                    op=ALU.add,
+                )
+                nc.sync.dma_start(
+                    out=outs[h][b, s * CHUNK : (s + 1) * CHUNK, 0, :].rearrange(
+                        "(p t) d -> p (t d)", t=ROWS_PER_PART
+                    ),
+                    in_=result[:, h].rearrange("p t d -> p (t d)"),
+                )
+
+        quantised = {}
+        projected = {}
+        with tc.manual_schedule():
+            for c in range(N_CHUNKS + 2):
+                if c + LOAD_AHEAD < N_CHUNKS:
+                    x_tiles[c + LOAD_AHEAD] = load(c + LOAD_AHEAD)
+                if c < N_CHUNKS:
+                    quantised[c] = turn_and_quantise(x_tiles[c])
+                if 1 <= c <= N_CHUNKS:
+                    codes, scales = quantised[c - 1]
+                    projected[c - 1] = project((c - 1) // BATCH, codes, scales)
+                if c >= 2:
+                    s, b = divmod(c - 2, BATCH)
+                    norm_rotate_store(s, b, projected[c - 2])

@@ -29,6 +29,8 @@ CHUNK = P * ROWS_PER_PART
 SEQ_CHUNKS = SEQ // CHUNK
 N_CHUNKS = BATCH * SEQ_CHUNKS
 LOAD_AHEAD = 3
+TABLE_PIECES = 4
+assert TABLE_PIECES == BATCH
 
 FLOPS = 2 * BATCH * SEQ * K * 2 * D
 
@@ -105,7 +107,8 @@ def tile_fluxjointattention_pa_t_kernel(
         w_words = const.tile([P, 4, PASSES, D], U32, align_bytes=64)
         w_scales = const.tile([P, 4, PASSES, D], U8, align_bytes=64)
         nc.vector.memset(w_scales[:].bitcast(I32), 0)
-        for w in (2, 3, 0, 1):
+
+        def load_weight(w):
             words, scales = weights[w]
             nc.sync.dma_start(
                 out=w_words[:, w].bitcast(I32),
@@ -117,6 +120,13 @@ def tile_fluxjointattention_pa_t_kernel(
                     out=w_scales[32 * q : 32 * q + 4, w].bitcast(I32),
                     in_=scale_rows[q].bitcast(I32),
                 )
+
+        load_weight(2)
+        load_weight(3)
+        for c in range(1, LOAD_AHEAD):
+            x_tiles[c] = load(c)
+        load_weight(0)
+        load_weight(1)
 
         bias_rows = const.tile([P, P], BF16)
         nc.vector.memset(bias_rows[:], 0.0)
@@ -148,30 +158,32 @@ def tile_fluxjointattention_pa_t_kernel(
 
         cos_rows = const.tile([P, SEQ_CHUNKS, ROWS_PER_PART, D], BF16)
         sin_rows = const.tile([P, SEQ_CHUNKS, ROWS_PER_PART, D], BF16)
-        for rows, table in ((cos_rows, rope_cos), (sin_rows, rope_sin)):
-            nc.scalar.dma_start(
-                out=rows[:].rearrange("p s t d -> p s (t d)"),
-                in_=table.rearrange("(s p t) d -> p s (t d)", s=SEQ_CHUNKS, t=ROWS_PER_PART),
-            )
-
-        for c in range(1, LOAD_AHEAD):
-            x_tiles[c] = load(c)
+        for part in (slice(0, 1), slice(1, SEQ_CHUNKS)):
+            for rows, table in ((cos_rows, rope_cos), (sin_rows, rope_sin)):
+                nc.scalar.dma_start(
+                    out=rows[:, part].rearrange("p s t d -> p s (t d)"),
+                    in_=table.rearrange("(s p t) d -> p s (t d)", s=SEQ_CHUNKS, t=ROWS_PER_PART)[:, part, :],
+                )
 
         table_c = const.tile([P, SEQ_CHUNKS, 2, ROWS_PER_PART, D], F32)
         table_s = const.tile([P, SEQ_CHUNKS, 2, ROWS_PER_PART, D], F32)
-        for s in range(SEQ_CHUNKS):
-            for h in range(2):
-                w = first_weight(s) + h
-                for table, rows, gain in ((table_c, cos_rows, gain_c), (table_s, sin_rows, gain_s)):
-                    nc.gpsimd.tensor_tensor(
-                        out=table[:, s, h].rearrange("p t (e i) -> p t e i", e=2),
-                        in0=rows[:, s].rearrange("p t (i e) -> p t e i", e=2),
-                        in1=gain[:, w]
-                        .rearrange("p (e i) -> p e i", e=2)
-                        .unsqueeze(1)
-                        .to_broadcast([P, ROWS_PER_PART, 2, HALF]),
-                        op=ALU.mult,
-                    )
+        table_kinds = ((table_c, cos_rows, gain_c), (table_s, sin_rows, gain_s))
+
+        def fill_table(s, piece):
+            h, kind = divmod(piece, 2)
+            table, rows, gain = table_kinds[kind]
+            nc.gpsimd.tensor_tensor(
+                out=table[:, s, h].rearrange("p t (e i) -> p t e i", e=2),
+                in0=rows[:, s].rearrange("p t (i e) -> p t e i", e=2),
+                in1=gain[:, first_weight(s) + h]
+                .rearrange("p (e i) -> p e i", e=2)
+                .unsqueeze(1)
+                .to_broadcast([P, ROWS_PER_PART, 2, HALF]),
+                op=ALU.mult,
+            )
+
+        for piece in range(TABLE_PIECES):
+            fill_table(0, piece)
 
         squares = const.tile([P, D], F32)
 
@@ -192,10 +204,13 @@ def tile_fluxjointattention_pa_t_kernel(
                                 in_=x_words[:, t, PASS_WORDS * g + u : PASS_WORDS * (g + 1) : 2],
                                 identity=ident[:],
                             )
-                    nc.scalar.copy(
+                    last_bank = g == PASSES - 1 and half == 1
+                    copy_out = nc.vector.tensor_copy if last_bank else nc.scalar.copy
+                    copy_out(
                         out=grouped_words[:, 2 * P * half : 2 * P * (half + 1), :],
                         in_=turned[:].rearrange("p u n -> p n u"),
                     )
+            for g in range(PASSES):
                 nc.vector.quantize_mx(
                     out=codes[:, g, :].bitcast(FP8X4), scales=scales[:, g, :], in_=grouped[:, g, :]
                 )
@@ -256,8 +271,7 @@ def tile_fluxjointattention_pa_t_kernel(
                         out=partner[:, h, t, HALF:D], in0=y[:, t, 0:HALF], scalar=r,
                         in1=table_s[:, s, h, t, HALF:D], op0=ALU.mult, op1=ALU.mult,
                     )
-            for h in range(2):
-                nc.vector.tensor_tensor(
+                nc.gpsimd.tensor_tensor(
                     out=result[:, h].rearrange("p t (i e) -> p t i e", e=2),
                     in0=own[:, h].rearrange("p t (e i) -> p t i e", e=2),
                     in1=partner[:, h].rearrange("p t (e i) -> p t i e", e=2),
@@ -276,6 +290,8 @@ def tile_fluxjointattention_pa_t_kernel(
             for c in range(N_CHUNKS + 2):
                 if c + LOAD_AHEAD < N_CHUNKS:
                     x_tiles[c + LOAD_AHEAD] = load(c + LOAD_AHEAD)
+                if c + BATCH < N_CHUNKS:
+                    fill_table(c // BATCH + 1, c % BATCH)
                 if c < N_CHUNKS:
                     quantised[c] = turn_and_quantise(x_tiles[c])
                 if 1 <= c <= N_CHUNKS:

@@ -73,7 +73,7 @@ def tile_fluxjointattention_pa_t_kernel(
         const = ctx.enter_context(tc.tile_pool(name="const", bufs=1))
         x_pool = ctx.enter_context(tc.tile_pool(name="x", bufs=LOAD_AHEAD + 1))
         work = ctx.enter_context(tc.tile_pool(name="work", bufs=2))
-        out_pool = ctx.enter_context(tc.tile_pool(name="out", bufs=3))
+        out_pool = ctx.enter_context(tc.tile_pool(name="out", bufs=4))
         turned_pool = ctx.enter_context(tc.psum_pool(name="turned", bufs=4))
         acc_pool = ctx.enter_context(tc.psum_pool(name="acc", bufs=2))
         back_pool = ctx.enter_context(tc.psum_pool(name="back", bufs=2))
@@ -187,102 +187,94 @@ def tile_fluxjointattention_pa_t_kernel(
 
         squares = const.tile([P, D], F32)
 
-        def turn_and_quantise(x_rows):
-            x_words = x_rows[:].bitcast(F32)
+        def new_quantised():
             grouped = work.tile([P, PASSES, 4 * CHUNK], BF16, align_bytes=64)
             codes = work.tile([P, PASSES, CHUNK], U32, align_bytes=64)
             scales = work.tile([P, PASSES, CHUNK], U8, align_bytes=64)
-            for g in range(PASSES):
-                grouped_words = grouped[:, g, :].bitcast(F32).rearrange("p (n u) -> p n u", u=2)
-                for half in range(2):
-                    turned = turned_pool.tile([P, 2, 2 * P], F32, tag="turned")
-                    for j in range(2):
-                        t = 2 * half + j
-                        for u in range(2):
-                            nc.tensor.transpose(
-                                out=turned[:, u, j * P : (j + 1) * P],
-                                in_=x_words[:, t, PASS_WORDS * g + u : PASS_WORDS * (g + 1) : 2],
-                                identity=ident[:],
-                            )
-                    last_bank = g == PASSES - 1 and half == 1
-                    copy_out = nc.vector.tensor_copy if last_bank else nc.scalar.copy
-                    copy_out(
-                        out=grouped_words[:, 2 * P * half : 2 * P * (half + 1), :],
-                        in_=turned[:].rearrange("p u n -> p n u"),
-                    )
-            for g in range(PASSES):
-                nc.vector.quantize_mx(
-                    out=codes[:, g, :].bitcast(FP8X4), scales=scales[:, g, :], in_=grouped[:, g, :]
-                )
-            return codes, scales
+            return grouped, codes, scales
 
-        def project(s, codes, scales):
-            y_cols = work.tile([P, 2, CHUNK], F32)
-            for h in range(2):
-                w = first_weight(s) + h
-                acc = acc_pool.tile([P, CHUNK], F32, tag="acc")
-                for g in range(PASSES):
-                    nc.tensor.matmul_mx(
-                        out=acc[:],
-                        lhsT=w_words[:, w, g, :].bitcast(FP8X4),
-                        lhsT_scale=w_scales[:, w, g, :],
-                        rhs=codes[:, g, :].bitcast(FP8X4),
-                        rhs_scale=scales[:, g, :],
-                        start=(g == 0),
-                        stop=(g == PASSES - 1),
-                    )
-                nc.scalar.activation(
-                    out=y_cols[:, h, :], in_=acc[:], func=ACT.Identity, bias=bias_col[:, w : w + 1], scale=1.0
+        def turn(x_rows, grouped, g):
+            x_words = x_rows[:].bitcast(F32)
+            grouped_words = grouped[:, g, :].bitcast(F32).rearrange("p (n u) -> p n u", u=2)
+            for half in range(2):
+                turned = turned_pool.tile([P, 2, 2 * P], F32, tag="turned")
+                for j in range(2):
+                    t = 2 * half + j
+                    for u in range(2):
+                        nc.tensor.transpose(
+                            out=turned[:, u, j * P : (j + 1) * P],
+                            in_=x_words[:, t, PASS_WORDS * g + u : PASS_WORDS * (g + 1) : 2],
+                            identity=ident[:],
+                        )
+                last_bank = g == PASSES - 1 and half == 1
+                copy_out = nc.vector.tensor_copy if last_bank else nc.scalar.copy
+                copy_out(
+                    out=grouped_words[:, 2 * P * half : 2 * P * (half + 1), :],
+                    in_=turned[:].rearrange("p u n -> p n u"),
                 )
-            return y_cols
 
-        def norm_rotate_store(s, b, y_cols):
-            sum_sq = work.tile([P, 2, ROWS_PER_PART], F32)
-            rms = work.tile([P, 2, ROWS_PER_PART], F32)
-            inv_rms = work.tile([P, 2, ROWS_PER_PART], F32)
-            own = work.tile([P, 2, ROWS_PER_PART, D], F32)
-            partner = work.tile([P, 2, ROWS_PER_PART, D], F32)
-            result = out_pool.tile([P, 2, ROWS_PER_PART, D], F32)
-            for h in range(2):
-                y = back_pool.tile([P, ROWS_PER_PART, D], F32)
-                for t in range(ROWS_PER_PART):
-                    nc.tensor.transpose(
-                        out=y[:, t, :], in_=y_cols[:, h, t * P : (t + 1) * P], identity=even_first[:]
-                    )
-                for t in range(ROWS_PER_PART):
-                    nc.scalar.activation(
-                        out=squares[:], in_=y[:, t, :], func=ACT.Square, accum_out=sum_sq[:, h, t : t + 1]
-                    )
+        def quantise(grouped, codes, scales, g):
+            nc.vector.quantize_mx(
+                out=codes[:, g, :].bitcast(FP8X4), scales=scales[:, g, :], in_=grouped[:, g, :]
+            )
+
+        def project(s, codes, scales, y_cols, h):
+            w = first_weight(s) + h
+            acc = acc_pool.tile([P, CHUNK], F32, tag="acc")
+            for g in range(PASSES):
+                nc.tensor.matmul_mx(
+                    out=acc[:],
+                    lhsT=w_words[:, w, g, :].bitcast(FP8X4),
+                    lhsT_scale=w_scales[:, w, g, :],
+                    rhs=codes[:, g, :].bitcast(FP8X4),
+                    rhs_scale=scales[:, g, :],
+                    start=(g == 0),
+                    stop=(g == PASSES - 1),
+                )
+            nc.scalar.activation(
+                out=y_cols[:, h, :], in_=acc[:], func=ACT.Identity, bias=bias_col[:, w : w + 1], scale=1.0
+            )
+
+        def norm_rotate_store(s, b, y_cols, h):
+            sum_sq = work.tile([P, ROWS_PER_PART], F32)
+            rms = work.tile([P, ROWS_PER_PART], F32)
+            inv_rms = work.tile([P, ROWS_PER_PART], F32)
+            own = work.tile([P, ROWS_PER_PART, D], F32)
+            partner = work.tile([P, ROWS_PER_PART, D], F32)
+            result = out_pool.tile([P, ROWS_PER_PART, D], F32)
+            y = back_pool.tile([P, ROWS_PER_PART, D], F32)
+            for t in range(ROWS_PER_PART):
+                nc.tensor.transpose(out=y[:, t, :], in_=y_cols[:, h, t * P : (t + 1) * P], identity=even_first[:])
+            for t in range(ROWS_PER_PART):
                 nc.scalar.activation(
-                    out=rms[:, h, :], in_=sum_sq[:, h, :], func=ACT.Sqrt, bias=eps[:, 0:1], scale=1.0 / D
+                    out=squares[:], in_=y[:, t, :], func=ACT.Square, accum_out=sum_sq[:, t : t + 1]
                 )
-                nc.vector.reciprocal(out=inv_rms[:, h, :], in_=rms[:, h, :])
-                for t in range(ROWS_PER_PART):
-                    r = inv_rms[:, h, t : t + 1]
-                    nc.vector.scalar_tensor_tensor(
-                        out=own[:, h, t, :], in0=y[:, t, :], scalar=r, in1=table_c[:, s, h, t, :],
-                        op0=ALU.mult, op1=ALU.mult,
-                    )
-                    nc.vector.scalar_tensor_tensor(
-                        out=partner[:, h, t, 0:HALF], in0=y[:, t, HALF:D], scalar=r,
-                        in1=table_s[:, s, h, t, 0:HALF], op0=ALU.mult, op1=ALU.mult,
-                    )
-                    nc.vector.scalar_tensor_tensor(
-                        out=partner[:, h, t, HALF:D], in0=y[:, t, 0:HALF], scalar=r,
-                        in1=table_s[:, s, h, t, HALF:D], op0=ALU.mult, op1=ALU.mult,
-                    )
-                nc.gpsimd.tensor_tensor(
-                    out=result[:, h].rearrange("p t (i e) -> p t i e", e=2),
-                    in0=own[:, h].rearrange("p t (e i) -> p t i e", e=2),
-                    in1=partner[:, h].rearrange("p t (e i) -> p t i e", e=2),
-                    op=ALU.add,
+            nc.scalar.activation(out=rms[:], in_=sum_sq[:], func=ACT.Sqrt, bias=eps[:, 0:1], scale=1.0 / D)
+            nc.vector.reciprocal(out=inv_rms[:], in_=rms[:])
+            for t in range(ROWS_PER_PART):
+                r = inv_rms[:, t : t + 1]
+                nc.vector.scalar_tensor_tensor(
+                    out=own[:, t, :], in0=y[:, t, :], scalar=r, in1=table_c[:, s, h, t, :],
+                    op0=ALU.mult, op1=ALU.mult,
                 )
-                nc.sync.dma_start(
-                    out=outs[h][b, s * CHUNK : (s + 1) * CHUNK, 0, :].rearrange(
-                        "(p t) d -> p (t d)", t=ROWS_PER_PART
-                    ),
-                    in_=result[:, h].rearrange("p t d -> p (t d)"),
+                nc.vector.scalar_tensor_tensor(
+                    out=partner[:, t, 0:HALF], in0=y[:, t, HALF:D], scalar=r,
+                    in1=table_s[:, s, h, t, 0:HALF], op0=ALU.mult, op1=ALU.mult,
                 )
+                nc.vector.scalar_tensor_tensor(
+                    out=partner[:, t, HALF:D], in0=y[:, t, 0:HALF], scalar=r,
+                    in1=table_s[:, s, h, t, HALF:D], op0=ALU.mult, op1=ALU.mult,
+                )
+            nc.gpsimd.tensor_tensor(
+                out=result[:].rearrange("p t (i e) -> p t i e", e=2),
+                in0=own[:].rearrange("p t (e i) -> p t i e", e=2),
+                in1=partner[:].rearrange("p t (e i) -> p t i e", e=2),
+                op=ALU.add,
+            )
+            nc.sync.dma_start(
+                out=outs[h][b, s * CHUNK : (s + 1) * CHUNK, 0, :].rearrange("(p t) d -> p (t d)", t=ROWS_PER_PART),
+                in_=result[:].rearrange("p t d -> p (t d)"),
+            )
 
         quantised = {}
         projected = {}
@@ -293,10 +285,18 @@ def tile_fluxjointattention_pa_t_kernel(
                 if c + BATCH < N_CHUNKS:
                     fill_table(c // BATCH + 1, c % BATCH)
                 if c < N_CHUNKS:
-                    quantised[c] = turn_and_quantise(x_tiles[c])
+                    quantised[c] = new_quantised()
                 if 1 <= c <= N_CHUNKS:
-                    codes, scales = quantised[c - 1]
-                    projected[c - 1] = project((c - 1) // BATCH, codes, scales)
-                if c >= 2:
-                    s, b = divmod(c - 2, BATCH)
-                    norm_rotate_store(s, b, projected[c - 2])
+                    projected[c - 1] = work.tile([P, 2, CHUNK], F32, name="y_cols")
+                for j in range(2):
+                    if c < N_CHUNKS:
+                        turn(x_tiles[c], quantised[c][0], j)
+                    if 1 <= c <= N_CHUNKS:
+                        grouped, codes, scales = quantised[c - 1]
+                        project((c - 1) // BATCH, codes, scales, projected[c - 1], j)
+                    if c >= 2:
+                        s, b = divmod(c - 2, BATCH)
+                        norm_rotate_store(s, b, projected[c - 2], j)
+                    if c < N_CHUNKS:
+                        grouped, codes, scales = quantised[c]
+                        quantise(grouped, codes, scales, j)

@@ -18,7 +18,6 @@ TEXT_ROWS = 512
 SEQ = 2048
 K = 1024
 D = 128
-HALF = D // 2
 EPS = 1e-6
 
 K_PASS = 4 * P
@@ -73,7 +72,7 @@ def tile_fluxjointattention_pa_t_kernel(
         const = ctx.enter_context(tc.tile_pool(name="const", bufs=1))
         x_pool = ctx.enter_context(tc.tile_pool(name="x", bufs=LOAD_AHEAD + 1))
         work = ctx.enter_context(tc.tile_pool(name="work", bufs=2))
-        out_pool = ctx.enter_context(tc.tile_pool(name="out", bufs=4))
+        out_pool = ctx.enter_context(tc.tile_pool(name="out", bufs=3))
         turned_pool = ctx.enter_context(tc.psum_pool(name="turned", bufs=4))
         acc_pool = ctx.enter_context(tc.psum_pool(name="acc", bufs=2))
         back_pool = ctx.enter_context(tc.psum_pool(name="back", bufs=2))
@@ -98,11 +97,6 @@ def tile_fluxjointattention_pa_t_kernel(
 
         ident = const.tile([P, P], F32)
         make_identity(nc, ident[:])
-        even_first = const.tile([P, P], F32)
-        nc.vector.tensor_copy(
-            out=even_first[:].rearrange("p (e i) -> p e i", e=2),
-            in_=ident[:].rearrange("p (i e) -> p e i", e=2),
-        )
 
         w_words = const.tile([P, 4, PASSES, D], U32, align_bytes=64)
         w_scales = const.tile([P, 4, PASSES, D], U8, align_bytes=64)
@@ -149,12 +143,13 @@ def tile_fluxjointattention_pa_t_kernel(
         nc.vector.memset(ones[:], 1.0)
         gain_all = acc_pool.tile([P, 4 * D], F32, tag="acc")
         nc.tensor.matmul(out=gain_all[:], lhsT=ones[:], rhs=gain_row[:], start=True, stop=True)
-        gain_pairs = gain_all[:].rearrange("p (w i e) -> p w e i", w=4, e=2)
         gain_c = const.tile([P, 4, D], F32)
-        nc.vector.tensor_copy(out=gain_c[:].rearrange("p w (e i) -> p w e i", e=2), in_=gain_pairs)
+        nc.vector.tensor_copy(out=gain_c[:].rearrange("p w d -> p (w d)"), in_=gain_all[:])
         gain_s = const.tile([P, 4, D], F32)
-        nc.vector.tensor_scalar_mul(out=gain_s[:, :, 0:HALF], in0=gain_pairs[:, :, 1, :], scalar1=-1.0)
-        nc.vector.tensor_copy(out=gain_s[:, :, HALF:D], in_=gain_pairs[:, :, 0, :])
+        gain_pairs = gain_all[:].rearrange("p (w i e) -> p w i e", w=4, e=2)
+        gain_s_pairs = gain_s[:].rearrange("p w (i e) -> p w i e", e=2)
+        nc.vector.tensor_scalar_mul(out=gain_s_pairs[:, :, :, 0], in0=gain_pairs[:, :, :, 1], scalar1=-1.0)
+        nc.vector.tensor_copy(out=gain_s_pairs[:, :, :, 1], in_=gain_pairs[:, :, :, 0])
 
         cos_rows = const.tile([P, SEQ_CHUNKS, ROWS_PER_PART, D], BF16)
         sin_rows = const.tile([P, SEQ_CHUNKS, ROWS_PER_PART, D], BF16)
@@ -173,12 +168,9 @@ def tile_fluxjointattention_pa_t_kernel(
             h, kind = divmod(piece, 2)
             table, rows, gain = table_kinds[kind]
             nc.gpsimd.tensor_tensor(
-                out=table[:, s, h].rearrange("p t (e i) -> p t e i", e=2),
-                in0=rows[:, s].rearrange("p t (i e) -> p t e i", e=2),
-                in1=gain[:, first_weight(s) + h]
-                .rearrange("p (e i) -> p e i", e=2)
-                .unsqueeze(1)
-                .to_broadcast([P, ROWS_PER_PART, 2, HALF]),
+                out=table[:, s, h],
+                in0=rows[:, s],
+                in1=gain[:, first_weight(s) + h].unsqueeze(1).to_broadcast([P, ROWS_PER_PART, D]),
                 op=ALU.mult,
             )
 
@@ -187,94 +179,94 @@ def tile_fluxjointattention_pa_t_kernel(
 
         squares = const.tile([P, D], F32)
 
-        def new_quantised():
+        def turn_and_quantise(x_rows):
+            x_words = x_rows[:].bitcast(F32)
             grouped = work.tile([P, PASSES, 4 * CHUNK], BF16, align_bytes=64)
             codes = work.tile([P, PASSES, CHUNK], U32, align_bytes=64)
             scales = work.tile([P, PASSES, CHUNK], U8, align_bytes=64)
-            return grouped, codes, scales
-
-        def turn(x_rows, grouped, g):
-            x_words = x_rows[:].bitcast(F32)
-            grouped_words = grouped[:, g, :].bitcast(F32).rearrange("p (n u) -> p n u", u=2)
-            for half in range(2):
-                turned = turned_pool.tile([P, 2, 2 * P], F32, tag="turned")
-                for j in range(2):
-                    t = 2 * half + j
-                    for u in range(2):
-                        nc.tensor.transpose(
-                            out=turned[:, u, j * P : (j + 1) * P],
-                            in_=x_words[:, t, PASS_WORDS * g + u : PASS_WORDS * (g + 1) : 2],
-                            identity=ident[:],
-                        )
-                last_bank = g == PASSES - 1 and half == 1
-                copy_out = nc.vector.tensor_copy if last_bank else nc.scalar.copy
-                copy_out(
-                    out=grouped_words[:, 2 * P * half : 2 * P * (half + 1), :],
-                    in_=turned[:].rearrange("p u n -> p n u"),
-                )
-
-        def quantise(grouped, codes, scales, g):
-            nc.vector.quantize_mx(
-                out=codes[:, g, :].bitcast(FP8X4), scales=scales[:, g, :], in_=grouped[:, g, :]
-            )
-
-        def project(s, codes, scales, y_cols, h):
-            w = first_weight(s) + h
-            acc = acc_pool.tile([P, CHUNK], F32, tag="acc")
             for g in range(PASSES):
-                nc.tensor.matmul_mx(
-                    out=acc[:],
-                    lhsT=w_words[:, w, g, :].bitcast(FP8X4),
-                    lhsT_scale=w_scales[:, w, g, :],
-                    rhs=codes[:, g, :].bitcast(FP8X4),
-                    rhs_scale=scales[:, g, :],
-                    start=(g == 0),
-                    stop=(g == PASSES - 1),
+                grouped_words = grouped[:, g, :].bitcast(F32).rearrange("p (n u) -> p n u", u=2)
+                for half in range(2):
+                    turned = turned_pool.tile([P, 2, 2 * P], F32, tag="turned")
+                    for j in range(2):
+                        t = 2 * half + j
+                        for u in range(2):
+                            nc.tensor.transpose(
+                                out=turned[:, u, j * P : (j + 1) * P],
+                                in_=x_words[:, t, PASS_WORDS * g + u : PASS_WORDS * (g + 1) : 2],
+                                identity=ident[:],
+                            )
+                    last_bank = g == PASSES - 1 and half == 1
+                    copy_out = nc.vector.tensor_copy if last_bank else nc.scalar.copy
+                    copy_out(
+                        out=grouped_words[:, 2 * P * half : 2 * P * (half + 1), :],
+                        in_=turned[:].rearrange("p u n -> p n u"),
+                    )
+            for g in range(PASSES):
+                nc.vector.quantize_mx(
+                    out=codes[:, g, :].bitcast(FP8X4), scales=scales[:, g, :], in_=grouped[:, g, :]
                 )
-            nc.scalar.activation(
-                out=y_cols[:, h, :], in_=acc[:], func=ACT.Identity, bias=bias_col[:, w : w + 1], scale=1.0
-            )
+            return codes, scales
 
-        def norm_rotate_store(s, b, y_cols, h):
-            sum_sq = work.tile([P, ROWS_PER_PART], F32)
-            rms = work.tile([P, ROWS_PER_PART], F32)
-            inv_rms = work.tile([P, ROWS_PER_PART], F32)
-            own = work.tile([P, ROWS_PER_PART, D], F32)
-            partner = work.tile([P, ROWS_PER_PART, D], F32)
-            result = out_pool.tile([P, ROWS_PER_PART, D], F32)
-            y = back_pool.tile([P, ROWS_PER_PART, D], F32)
-            for t in range(ROWS_PER_PART):
-                nc.tensor.transpose(out=y[:, t, :], in_=y_cols[:, h, t * P : (t + 1) * P], identity=even_first[:])
-            for t in range(ROWS_PER_PART):
+        def project(s, codes, scales):
+            y_cols = work.tile([P, 2, CHUNK], F32)
+            for h in range(2):
+                w = first_weight(s) + h
+                acc = acc_pool.tile([P, CHUNK], F32, tag="acc")
+                for g in range(PASSES):
+                    nc.tensor.matmul_mx(
+                        out=acc[:],
+                        lhsT=w_words[:, w, g, :].bitcast(FP8X4),
+                        lhsT_scale=w_scales[:, w, g, :],
+                        rhs=codes[:, g, :].bitcast(FP8X4),
+                        rhs_scale=scales[:, g, :],
+                        start=(g == 0),
+                        stop=(g == PASSES - 1),
+                    )
                 nc.scalar.activation(
-                    out=squares[:], in_=y[:, t, :], func=ACT.Square, accum_out=sum_sq[:, t : t + 1]
+                    out=y_cols[:, h, :], in_=acc[:], func=ACT.Identity, bias=bias_col[:, w : w + 1], scale=1.0
                 )
-            nc.scalar.activation(out=rms[:], in_=sum_sq[:], func=ACT.Sqrt, bias=eps[:, 0:1], scale=1.0 / D)
-            nc.vector.reciprocal(out=inv_rms[:], in_=rms[:])
-            for t in range(ROWS_PER_PART):
-                r = inv_rms[:, t : t + 1]
-                nc.vector.scalar_tensor_tensor(
-                    out=own[:, t, :], in0=y[:, t, :], scalar=r, in1=table_c[:, s, h, t, :],
-                    op0=ALU.mult, op1=ALU.mult,
+            return y_cols
+
+        def norm_rotate_store(s, b, y_cols):
+            sum_sq = work.tile([P, 2, ROWS_PER_PART], F32)
+            rms = work.tile([P, 2, ROWS_PER_PART], F32)
+            inv_rms = work.tile([P, 2, ROWS_PER_PART], F32)
+            own = work.tile([P, 2, ROWS_PER_PART, D], F32)
+            partner = work.tile([P, 2, ROWS_PER_PART, D], F32)
+            result = out_pool.tile([P, 2, ROWS_PER_PART, D], F32)
+            for h in range(2):
+                y = back_pool.tile([P, ROWS_PER_PART, D], F32)
+                for t in range(ROWS_PER_PART):
+                    nc.tensor.transpose(out=y[:, t, :], in_=y_cols[:, h, t * P : (t + 1) * P], identity=ident[:])
+                for t in range(ROWS_PER_PART):
+                    nc.scalar.activation(
+                        out=squares[:], in_=y[:, t, :], func=ACT.Square, accum_out=sum_sq[:, h, t : t + 1]
+                    )
+                nc.scalar.activation(
+                    out=rms[:, h, :], in_=sum_sq[:, h, :], func=ACT.Sqrt, bias=eps[:, 0:1], scale=1.0 / D
                 )
-                nc.vector.scalar_tensor_tensor(
-                    out=partner[:, t, 0:HALF], in0=y[:, t, HALF:D], scalar=r,
-                    in1=table_s[:, s, h, t, 0:HALF], op0=ALU.mult, op1=ALU.mult,
+                nc.vector.reciprocal(out=inv_rms[:, h, :], in_=rms[:, h, :])
+                for t in range(ROWS_PER_PART):
+                    r = inv_rms[:, h, t : t + 1]
+                    nc.vector.scalar_tensor_tensor(
+                        out=own[:, h, t, :], in0=y[:, t, :], scalar=r, in1=table_c[:, s, h, t, :],
+                        op0=ALU.mult, op1=ALU.mult,
+                    )
+                    nc.vector.scalar_tensor_tensor(
+                        out=partner[:, h, t, :].rearrange("p (i e) -> p i e", e=2),
+                        in0=y[:, t, :].rearrange("p (i e) -> p i e", e=2)[:, :, ::-1],
+                        scalar=r,
+                        in1=table_s[:, s, h, t, :].rearrange("p (i e) -> p i e", e=2),
+                        op0=ALU.mult, op1=ALU.mult,
+                    )
+                nc.gpsimd.tensor_tensor(out=result[:, h], in0=own[:, h], in1=partner[:, h], op=ALU.add)
+                nc.sync.dma_start(
+                    out=outs[h][b, s * CHUNK : (s + 1) * CHUNK, 0, :].rearrange(
+                        "(p t) d -> p (t d)", t=ROWS_PER_PART
+                    ),
+                    in_=result[:, h].rearrange("p t d -> p (t d)"),
                 )
-                nc.vector.scalar_tensor_tensor(
-                    out=partner[:, t, HALF:D], in0=y[:, t, 0:HALF], scalar=r,
-                    in1=table_s[:, s, h, t, HALF:D], op0=ALU.mult, op1=ALU.mult,
-                )
-            nc.gpsimd.tensor_tensor(
-                out=result[:].rearrange("p t (i e) -> p t i e", e=2),
-                in0=own[:].rearrange("p t (e i) -> p t i e", e=2),
-                in1=partner[:].rearrange("p t (e i) -> p t i e", e=2),
-                op=ALU.add,
-            )
-            nc.sync.dma_start(
-                out=outs[h][b, s * CHUNK : (s + 1) * CHUNK, 0, :].rearrange("(p t) d -> p (t d)", t=ROWS_PER_PART),
-                in_=result[:].rearrange("p t d -> p (t d)"),
-            )
 
         quantised = {}
         projected = {}
@@ -285,18 +277,10 @@ def tile_fluxjointattention_pa_t_kernel(
                 if c + BATCH < N_CHUNKS:
                     fill_table(c // BATCH + 1, c % BATCH)
                 if c < N_CHUNKS:
-                    quantised[c] = new_quantised()
+                    quantised[c] = turn_and_quantise(x_tiles[c])
                 if 1 <= c <= N_CHUNKS:
-                    projected[c - 1] = work.tile([P, 2, CHUNK], F32, name="y_cols")
-                for j in range(2):
-                    if c < N_CHUNKS:
-                        turn(x_tiles[c], quantised[c][0], j)
-                    if 1 <= c <= N_CHUNKS:
-                        grouped, codes, scales = quantised[c - 1]
-                        project((c - 1) // BATCH, codes, scales, projected[c - 1], j)
-                    if c >= 2:
-                        s, b = divmod(c - 2, BATCH)
-                        norm_rotate_store(s, b, projected[c - 2], j)
-                    if c < N_CHUNKS:
-                        grouped, codes, scales = quantised[c]
-                        quantise(grouped, codes, scales, j)
+                    codes, scales = quantised[c - 1]
+                    projected[c - 1] = project((c - 1) // BATCH, codes, scales)
+                if c >= 2:
+                    s, b = divmod(c - 2, BATCH)
+                    norm_rotate_store(s, b, projected[c - 2])

@@ -93,7 +93,7 @@ def tile_fluxjointattention_pa_t_kernel(
         eps = const.tile([P, 1], F32)
         nc.vector.memset(eps[:], EPS)
         warm = const.tile([P, 1], F32)
-        nc.scalar.activation(out=warm[:], in_=eps[:], func=ACT.Sqrt)
+        nc.scalar.activation(out=warm[:], in_=eps[:], func=ACT.Abs_reciprocal_sqrt)
 
         ident = const.tile([P, P], F32)
         make_identity(nc, ident[:])
@@ -202,10 +202,11 @@ def tile_fluxjointattention_pa_t_kernel(
                         out=grouped_words[:, 2 * P * half : 2 * P * (half + 1), :],
                         in_=turned[:].rearrange("p u n -> p n u"),
                     )
-            for g in range(PASSES):
-                nc.vector.quantize_mx(
-                    out=codes[:, g, :].bitcast(FP8X4), scales=scales[:, g, :], in_=grouped[:, g, :]
-                )
+            nc.vector.quantize_mx(
+                out=codes[:].rearrange("p g n -> p (g n)").bitcast(FP8X4),
+                scales=scales[:].rearrange("p g n -> p (g n)"),
+                in_=grouped[:].rearrange("p g n -> p (g n)"),
+            )
             return codes, scales
 
         def project(s, codes, scales):
@@ -230,7 +231,6 @@ def tile_fluxjointattention_pa_t_kernel(
 
         def norm_rotate_store(s, b, y_cols):
             sum_sq = work.tile([P, 2, ROWS_PER_PART], F32)
-            rms = work.tile([P, 2, ROWS_PER_PART], F32)
             inv_rms = work.tile([P, 2, ROWS_PER_PART], F32)
             own = work.tile([P, 2, ROWS_PER_PART, D], F32)
             partner = work.tile([P, 2, ROWS_PER_PART, D], F32)
@@ -244,9 +244,9 @@ def tile_fluxjointattention_pa_t_kernel(
                         out=squares[:], in_=y[:, t, :], func=ACT.Square, accum_out=sum_sq[:, h, t : t + 1]
                     )
                 nc.scalar.activation(
-                    out=rms[:, h, :], in_=sum_sq[:, h, :], func=ACT.Sqrt, bias=eps[:, 0:1], scale=1.0 / D
+                    out=inv_rms[:, h, :], in_=sum_sq[:, h, :], func=ACT.Abs_reciprocal_sqrt,
+                    bias=eps[:, 0:1], scale=1.0 / D,
                 )
-                nc.vector.reciprocal(out=inv_rms[:, h, :], in_=rms[:, h, :])
                 for t in range(ROWS_PER_PART):
                     r = inv_rms[:, h, t : t + 1]
                     nc.vector.scalar_tensor_tensor(

@@ -177,7 +177,6 @@ def tile_fluxjointattention_pa_t_kernel(
         for piece in range(TABLE_PIECES):
             fill_table(0, piece)
 
-        squares = const.tile([P, D], F32)
 
         def turn_and_quantise(x_rows):
             x_words = x_rows[:].bitcast(F32)
@@ -232,6 +231,7 @@ def tile_fluxjointattention_pa_t_kernel(
         def norm_rotate_store(s, b, y_cols):
             sum_sq = work.tile([P, 2, ROWS_PER_PART], F32)
             inv_rms = work.tile([P, 2, ROWS_PER_PART], F32)
+            squares = work.tile([P, 2, ROWS_PER_PART, D], F32)
             own = work.tile([P, 2, ROWS_PER_PART, D], F32)
             partner = work.tile([P, 2, ROWS_PER_PART, D], F32)
             result = out_pool.tile([P, 2, ROWS_PER_PART, D], F32)
@@ -241,7 +241,7 @@ def tile_fluxjointattention_pa_t_kernel(
                     nc.tensor.transpose(out=y[:, t, :], in_=y_cols[:, h, t * P : (t + 1) * P], identity=ident[:])
                 for t in range(ROWS_PER_PART):
                     nc.scalar.activation(
-                        out=squares[:], in_=y[:, t, :], func=ACT.Square, accum_out=sum_sq[:, h, t : t + 1]
+                        out=squares[:, h, t, :], in_=y[:, t, :], func=ACT.Square, accum_out=sum_sq[:, h, t : t + 1]
                     )
                 nc.scalar.activation(
                     out=inv_rms[:, h, :], in_=sum_sq[:, h, :], func=ACT.Abs_reciprocal_sqrt,

@@ -148,8 +148,8 @@ def tile_fluxjointattention_pa_t_kernel(
         gain_s = const.tile([P, 4, D], F32)
         gain_pairs = gain_all[:].rearrange("p (w i e) -> p w i e", w=4, e=2)
         gain_s_pairs = gain_s[:].rearrange("p w (i e) -> p w i e", e=2)
-        nc.vector.tensor_scalar_mul(out=gain_s_pairs[:, :, :, 0], in0=gain_pairs[:, :, :, 1], scalar1=-1.0)
-        nc.vector.tensor_copy(out=gain_s_pairs[:, :, :, 1], in_=gain_pairs[:, :, :, 0])
+        nc.vector.tensor_copy(out=gain_s_pairs[:, :, :, 0], in_=gain_pairs[:, :, :, 0])
+        nc.vector.tensor_scalar_mul(out=gain_s_pairs[:, :, :, 1], in0=gain_pairs[:, :, :, 1], scalar1=-1.0)
 
         cos_rows = const.tile([P, SEQ_CHUNKS, ROWS_PER_PART, D], BF16)
         sin_rows = const.tile([P, SEQ_CHUNKS, ROWS_PER_PART, D], BF16)
@@ -160,17 +160,22 @@ def tile_fluxjointattention_pa_t_kernel(
                     in_=table.rearrange("(s p t) d -> p s (t d)", s=SEQ_CHUNKS, t=ROWS_PER_PART)[:, part, :],
                 )
 
-        table_c = const.tile([P, SEQ_CHUNKS, 2, ROWS_PER_PART, D], F32)
-        table_s = const.tile([P, SEQ_CHUNKS, 2, ROWS_PER_PART, D], F32)
-        table_kinds = ((table_c, cos_rows, gain_c), (table_s, sin_rows, gain_s))
+        tables = const.tile([P, SEQ_CHUNKS, 2, ROWS_PER_PART, 2, D], F32)
+
+        def pairs(ap):
+            return ap.rearrange("p t (i e) -> p t i e", e=2)
 
         def fill_table(s, piece):
             h, kind = divmod(piece, 2)
-            table, rows, gain = table_kinds[kind]
+            w = first_weight(s) + h
+            if kind == 0:
+                rows, gain = pairs(cos_rows[:, s]), gain_c
+            else:
+                rows, gain = pairs(sin_rows[:, s])[:, :, :, ::-1], gain_s
             nc.gpsimd.tensor_tensor(
-                out=table[:, s, h],
-                in0=rows[:, s],
-                in1=gain[:, first_weight(s) + h].unsqueeze(1).to_broadcast([P, ROWS_PER_PART, D]),
+                out=pairs(tables[:, s, h, :, kind, :]),
+                in0=rows,
+                in1=pairs(gain[:, w].unsqueeze(1).to_broadcast([P, ROWS_PER_PART, D])),
                 op=ALU.mult,
             )
 
@@ -232,8 +237,7 @@ def tile_fluxjointattention_pa_t_kernel(
             sum_sq = work.tile([P, 2, ROWS_PER_PART], F32)
             inv_rms = work.tile([P, 2, ROWS_PER_PART], F32)
             squares = work.tile([P, 2, ROWS_PER_PART, D], F32)
-            own = work.tile([P, 2, ROWS_PER_PART, D], F32)
-            partner = work.tile([P, 2, ROWS_PER_PART, D], F32)
+            products = work.tile([P, 2, ROWS_PER_PART, 2, D], F32)
             result = out_pool.tile([P, 2, ROWS_PER_PART, D], F32)
             for h in range(2):
                 y = back_pool.tile([P, ROWS_PER_PART, D], F32)
@@ -250,17 +254,13 @@ def tile_fluxjointattention_pa_t_kernel(
                 for t in range(ROWS_PER_PART):
                     r = inv_rms[:, h, t : t + 1]
                     nc.vector.scalar_tensor_tensor(
-                        out=own[:, h, t, :], in0=y[:, t, :], scalar=r, in1=table_c[:, s, h, t, :],
-                        op0=ALU.mult, op1=ALU.mult,
+                        out=products[:, h, t], in0=y[:, t, :].unsqueeze(1).to_broadcast([P, 2, D]), scalar=r,
+                        in1=tables[:, s, h, t], op0=ALU.mult, op1=ALU.mult,
                     )
-                    nc.vector.scalar_tensor_tensor(
-                        out=partner[:, h, t, :].rearrange("p (i e) -> p i e", e=2),
-                        in0=y[:, t, :].rearrange("p (i e) -> p i e", e=2)[:, :, ::-1],
-                        scalar=r,
-                        in1=table_s[:, s, h, t, :].rearrange("p (i e) -> p i e", e=2),
-                        op0=ALU.mult, op1=ALU.mult,
-                    )
-                nc.gpsimd.tensor_tensor(out=result[:, h], in0=own[:, h], in1=partner[:, h], op=ALU.add)
+                nc.gpsimd.tensor_tensor(
+                    out=pairs(result[:, h]), in0=pairs(products[:, h, :, 0, :]),
+                    in1=pairs(products[:, h, :, 1, :])[:, :, :, ::-1], op=ALU.add,
+                )
                 nc.sync.dma_start(
                     out=outs[h][b, s * CHUNK : (s + 1) * CHUNK, 0, :].rearrange(
                         "(p t) d -> p (t d)", t=ROWS_PER_PART

@@ -233,14 +233,16 @@ def tile_fluxjointattention_pa_t_kernel(
                 )
             return y_cols
 
-        def norm_rotate_store(s, b, y_cols):
+        def norm_rotate_store(s, b, y_cols, between):
             sum_sq = work.tile([P, 2, ROWS_PER_PART], F32)
             inv_rms = work.tile([P, 2, ROWS_PER_PART], F32)
             squares = work.tile([P, 2, ROWS_PER_PART, D], F32)
             products = work.tile([P, 2, ROWS_PER_PART, 2, D], F32)
             result = out_pool.tile([P, 2, ROWS_PER_PART, D], F32)
+            ys = []
             for h in range(2):
                 y = back_pool.tile([P, ROWS_PER_PART, D], F32)
+                ys.append(y)
                 for t in range(ROWS_PER_PART):
                     nc.tensor.transpose(out=y[:, t, :], in_=y_cols[:, h, t * P : (t + 1) * P], identity=ident[:])
                 for t in range(ROWS_PER_PART):
@@ -251,16 +253,21 @@ def tile_fluxjointattention_pa_t_kernel(
                     out=inv_rms[:, h, :], in_=sum_sq[:, h, :], func=ACT.Abs_reciprocal_sqrt,
                     bias=eps[:, 0:1], scale=1.0 / D,
                 )
+            between()
+            for h in range(2):
+                y = ys[h]
                 for t in range(ROWS_PER_PART):
                     r = inv_rms[:, h, t : t + 1]
                     nc.vector.scalar_tensor_tensor(
                         out=products[:, h, t], in0=y[:, t, :].unsqueeze(1).to_broadcast([P, 2, D]), scalar=r,
                         in1=tables[:, s, h, t], op0=ALU.mult, op1=ALU.mult,
                     )
-                nc.gpsimd.tensor_tensor(
-                    out=pairs(result[:, h]), in0=pairs(products[:, h, :, 0, :]),
-                    in1=pairs(products[:, h, :, 1, :])[:, :, :, ::-1], op=ALU.add,
-                )
+                    first = {(0, ROWS_PER_PART - 1): 0, (1, 1): 0, (1, ROWS_PER_PART - 1): 2}.get((h, t))
+                    if first is not None:
+                        nc.gpsimd.tensor_tensor(
+                            out=pairs(result[:, h, first : t + 1]), in0=pairs(products[:, h, first : t + 1, 0, :]),
+                            in1=pairs(products[:, h, first : t + 1, 1, :])[:, :, :, ::-1], op=ALU.add,
+                        )
                 nc.sync.dma_start(
                     out=outs[h][b, s * CHUNK : (s + 1) * CHUNK, 0, :].rearrange(
                         "(p t) d -> p (t d)", t=ROWS_PER_PART
@@ -278,9 +285,12 @@ def tile_fluxjointattention_pa_t_kernel(
                     fill_table(c // BATCH + 1, c % BATCH)
                 if c < N_CHUNKS:
                     quantised[c] = turn_and_quantise(x_tiles[c])
-                if 1 <= c <= N_CHUNKS:
-                    codes, scales = quantised[c - 1]
-                    projected[c - 1] = project((c - 1) // BATCH, codes, scales)
+                def project_last():
+                    if 1 <= c <= N_CHUNKS:
+                        projected[c - 1] = project((c - 1) // BATCH, quantised[c - 1][0], quantised[c - 1][1])
+
                 if c >= 2:
                     s, b = divmod(c - 2, BATCH)
-                    norm_rotate_store(s, b, projected[c - 2])
+                    norm_rotate_store(s, b, projected[c - 2], project_last)
+                else:
+                    project_last()

@@ -115,10 +115,10 @@ def tile_fluxjointattention_pa_t_kernel(
                     in_=scale_rows[q].bitcast(I32),
                 )
 
+        x_tiles[1] = load(1)
         load_weight(2)
         load_weight(3)
-        for c in range(1, LOAD_AHEAD):
-            x_tiles[c] = load(c)
+        x_tiles[2] = load(2)
         load_weight(0)
         load_weight(1)
 
@@ -233,7 +233,7 @@ def tile_fluxjointattention_pa_t_kernel(
                 )
             return y_cols
 
-        def norm_rotate_store(s, b, y_cols, between):
+        def norm_rotate_store(s, b, y_cols, between, last_chunk):
             sum_sq = work.tile([P, 2, ROWS_PER_PART], F32)
             inv_rms = work.tile([P, 2, ROWS_PER_PART], F32)
             squares = work.tile([P, 2, ROWS_PER_PART, D], F32)
@@ -264,7 +264,9 @@ def tile_fluxjointattention_pa_t_kernel(
                     )
                     first = {(0, ROWS_PER_PART - 1): 0, (1, 1): 0, (1, ROWS_PER_PART - 1): 2}.get((h, t))
                     if first is not None:
-                        nc.gpsimd.tensor_tensor(
+                        very_last = last_chunk and h == 1 and t == ROWS_PER_PART - 1
+                        adder = nc.vector if very_last else nc.gpsimd
+                        adder.tensor_tensor(
                             out=pairs(result[:, h, first : t + 1]), in0=pairs(products[:, h, first : t + 1, 0, :]),
                             in1=pairs(products[:, h, first : t + 1, 1, :])[:, :, :, ::-1], op=ALU.add,
                         )
@@ -291,6 +293,6 @@ def tile_fluxjointattention_pa_t_kernel(
 
                 if c >= 2:
                     s, b = divmod(c - 2, BATCH)
-                    norm_rotate_store(s, b, projected[c - 2], project_last)
+                    norm_rotate_store(s, b, projected[c - 2], project_last, c - 2 == N_CHUNKS - 1)
                 else:
                     project_last()

@@ -31,6 +31,11 @@ LOAD_AHEAD = 3
 TABLE_PIECES = 4
 assert TABLE_PIECES == BATCH
 
+PASS_MAJOR = [(0, 0), (0, 1), (1, 0), (1, 1)]
+HALF_MAJOR = [(0, 0), (1, 0), (0, 1), (1, 1)]
+
+ADD_FIRST = {(0, 3): 0, (1, 1): 0, (1, 3): 2}
+
 FLOPS = 2 * BATCH * SEQ * K * 2 * D
 
 
@@ -77,23 +82,28 @@ def tile_fluxjointattention_pa_t_kernel(
         acc_pool = ctx.enter_context(tc.psum_pool(name="acc", bufs=2))
         back_pool = ctx.enter_context(tc.psum_pool(name="back", bufs=2))
 
-        def load(c):
+        def load(c, pieces=1):
             s, b = divmod(c, BATCH)
             if s == 0:
                 rows = encoder_hidden_states[b]
             else:
                 rows = hidden_states[b, (s - 1) * CHUNK : s * CHUNK, :]
             x_rows = x_pool.tile([P, ROWS_PER_PART, K], BF16)
-            nc.sync.dma_start(out=x_rows[:], in_=rows.rearrange("(p t) k -> p t k", t=ROWS_PER_PART))
+            by_part = rows.rearrange("(p t) k -> p t k", t=ROWS_PER_PART)
+            step = ROWS_PER_PART // pieces
+            for t in range(0, ROWS_PER_PART, step):
+                nc.sync.dma_start(out=x_rows[:, t : t + step, :], in_=by_part[:, t : t + step, :])
             return x_rows
 
         x_tiles = {}
-        x_tiles[0] = load(0)
+        x_tiles[0] = load(0, pieces=2)
 
+        bias_rows = const.tile([P, P], BF16)
+        nc.vector.memset(bias_rows[:], 0.0)
+        gain_row = const.tile([P, 4 * D], BF16)
+        nc.vector.memset(gain_row[:], 0.0)
         eps = const.tile([P, 1], F32)
         nc.vector.memset(eps[:], EPS)
-        warm = const.tile([P, 1], F32)
-        nc.scalar.activation(out=warm[:], in_=eps[:], func=ACT.Abs_reciprocal_sqrt)
 
         ident = const.tile([P, P], F32)
         make_identity(nc, ident[:])
@@ -115,50 +125,52 @@ def tile_fluxjointattention_pa_t_kernel(
                     in_=scale_rows[q].bitcast(I32),
                 )
 
+        for w in range(4):
+            nc.scalar.dma_start(out=bias_rows[w : w + 1, :], in_=biases[w].rearrange("(o d) -> o d", o=1))
+        warm = const.tile([P, 1], F32)
+        nc.scalar.activation(out=warm[:], in_=eps[:], func=ACT.Abs_reciprocal_sqrt)
+        bias_rows32 = const.tile([P, P], F32)
+        bias_col = const.tile([P, 4], F32)
+
+        for w in range(4):
+            nc.gpsimd.dma_start(
+                out=gain_row[0:1, w * D : (w + 1) * D], in_=gains[w].rearrange("(o d) -> o d", o=1)
+            )
+        ones = const.tile([P, P], BF16)
+        nc.vector.memset(ones[:], 1.0)
+        gain_c = const.tile([P, 4, D], F32)
+        gain_s = const.tile([P, 4, D], F32)
+
+        def spread_biases_and_gains():
+            nc.gpsimd.tensor_copy(out=bias_rows32[:], in_=bias_rows[:])
+            bias_turned = back_pool.tile([P, 4 * D], F32, tag="back")
+            nc.tensor.transpose(out=bias_turned[:, 0:P], in_=bias_rows32[:], identity=ident[:])
+            gain_all = back_pool.tile([P, 4 * D], F32, tag="back")
+            nc.tensor.matmul(out=gain_all[:], lhsT=ones[:], rhs=gain_row[:], start=True, stop=True)
+            nc.vector.tensor_copy(out=bias_col[:], in_=bias_turned[:, 0:4])
+            nc.vector.tensor_copy(out=gain_c[:].rearrange("p w d -> p (w d)"), in_=gain_all[:])
+            gain_pairs = gain_all[:].rearrange("p (w i e) -> p w i e", w=4, e=2)
+            gain_s_pairs = gain_s[:].rearrange("p w (i e) -> p w i e", e=2)
+            nc.vector.tensor_copy(out=gain_s_pairs[:, :, :, 0], in_=gain_pairs[:, :, :, 0])
+            nc.vector.tensor_scalar_mul(out=gain_s_pairs[:, :, :, 1], in0=gain_pairs[:, :, :, 1], scalar1=-1.0)
+
+        cos_rows = const.tile([P, SEQ_CHUNKS, ROWS_PER_PART, D], BF16)
+        sin_rows = const.tile([P, SEQ_CHUNKS, ROWS_PER_PART, D], BF16)
+
+        def load_rotary(queue, part):
+            for rows, table in ((cos_rows, rope_cos), (sin_rows, rope_sin)):
+                queue.dma_start(
+                    out=rows[:, part].rearrange("p s t d -> p s (t d)"),
+                    in_=table.rearrange("(s p t) d -> p s (t d)", s=SEQ_CHUNKS, t=ROWS_PER_PART)[:, part, :],
+                )
+
         x_tiles[1] = load(1)
+        load_rotary(nc.sync, slice(0, 1))
         load_weight(2)
         load_weight(3)
         x_tiles[2] = load(2)
         load_weight(0)
         load_weight(1)
-
-        bias_rows = const.tile([P, P], BF16)
-        nc.vector.memset(bias_rows[:], 0.0)
-        for w in range(4):
-            nc.scalar.dma_start(out=bias_rows[w : w + 1, :], in_=biases[w].rearrange("(o d) -> o d", o=1))
-        bias_rows32 = const.tile([P, P], F32)
-        nc.vector.tensor_copy(out=bias_rows32[:], in_=bias_rows[:])
-        bias_turned = turned_pool.tile([P, 2, 2 * P], F32, tag="turned")
-        nc.tensor.transpose(out=bias_turned[:, 0, 0:P], in_=bias_rows32[:], identity=ident[:])
-        bias_col = const.tile([P, 4], F32)
-        nc.vector.tensor_copy(out=bias_col[:], in_=bias_turned[:, 0, 0:4])
-
-        gain_row = const.tile([P, 4 * D], BF16)
-        nc.vector.memset(gain_row[:], 0.0)
-        for w in range(4):
-            nc.scalar.dma_start(
-                out=gain_row[0:1, w * D : (w + 1) * D], in_=gains[w].rearrange("(o d) -> o d", o=1)
-            )
-        ones = const.tile([P, P], BF16)
-        nc.vector.memset(ones[:], 1.0)
-        gain_all = acc_pool.tile([P, 4 * D], F32, tag="acc")
-        nc.tensor.matmul(out=gain_all[:], lhsT=ones[:], rhs=gain_row[:], start=True, stop=True)
-        gain_c = const.tile([P, 4, D], F32)
-        nc.vector.tensor_copy(out=gain_c[:].rearrange("p w d -> p (w d)"), in_=gain_all[:])
-        gain_s = const.tile([P, 4, D], F32)
-        gain_pairs = gain_all[:].rearrange("p (w i e) -> p w i e", w=4, e=2)
-        gain_s_pairs = gain_s[:].rearrange("p w (i e) -> p w i e", e=2)
-        nc.vector.tensor_copy(out=gain_s_pairs[:, :, :, 0], in_=gain_pairs[:, :, :, 0])
-        nc.vector.tensor_scalar_mul(out=gain_s_pairs[:, :, :, 1], in0=gain_pairs[:, :, :, 1], scalar1=-1.0)
-
-        cos_rows = const.tile([P, SEQ_CHUNKS, ROWS_PER_PART, D], BF16)
-        sin_rows = const.tile([P, SEQ_CHUNKS, ROWS_PER_PART, D], BF16)
-        for part in (slice(0, 1), slice(1, SEQ_CHUNKS)):
-            for rows, table in ((cos_rows, rope_cos), (sin_rows, rope_sin)):
-                nc.scalar.dma_start(
-                    out=rows[:, part].rearrange("p s t d -> p s (t d)"),
-                    in_=table.rearrange("(s p t) d -> p s (t d)", s=SEQ_CHUNKS, t=ROWS_PER_PART)[:, part, :],
-                )
 
         tables = const.tile([P, SEQ_CHUNKS, 2, ROWS_PER_PART, 2, D], F32)
 
@@ -179,120 +191,141 @@ def tile_fluxjointattention_pa_t_kernel(
                 op=ALU.mult,
             )
 
-        for piece in range(TABLE_PIECES):
-            fill_table(0, piece)
 
+        grouped, codes, scales = {}, {}, {}
+        y_cols, ys, sum_sq, inv_rms, squares, products, result = {}, {}, {}, {}, {}, {}, {}
 
-        def turn_and_quantise(x_rows):
-            x_words = x_rows[:].bitcast(F32)
-            grouped = work.tile([P, PASSES, 4 * CHUNK], BF16, align_bytes=64)
-            codes = work.tile([P, PASSES, CHUNK], U32, align_bytes=64)
-            scales = work.tile([P, PASSES, CHUNK], U8, align_bytes=64)
-            for g in range(PASSES):
-                grouped_words = grouped[:, g, :].bitcast(F32).rearrange("p (n u) -> p n u", u=2)
-                for half in range(2):
-                    turned = turned_pool.tile([P, 2, 2 * P], F32, tag="turned")
-                    for j in range(2):
-                        t = 2 * half + j
-                        for u in range(2):
-                            nc.tensor.transpose(
-                                out=turned[:, u, j * P : (j + 1) * P],
-                                in_=x_words[:, t, PASS_WORDS * g + u : PASS_WORDS * (g + 1) : 2],
-                                identity=ident[:],
-                            )
-                    last_bank = g == PASSES - 1 and half == 1
-                    copy_out = nc.vector.tensor_copy if last_bank else nc.scalar.copy
-                    copy_out(
-                        out=grouped_words[:, 2 * P * half : 2 * P * (half + 1), :],
-                        in_=turned[:].rearrange("p u n -> p n u"),
+        def open_chunk(c):
+            grouped[c] = work.tile([P, PASSES, 4 * CHUNK], BF16, align_bytes=64, name="grouped")
+            codes[c] = work.tile([P, PASSES, CHUNK], U32, align_bytes=64, name="codes")
+            scales[c] = work.tile([P, PASSES, CHUNK], U8, align_bytes=64, name="scales")
+
+        def turn(c, bank, copy_out):
+            g, half = bank
+            x_words = x_tiles[c][:].bitcast(F32)
+            turned = turned_pool.tile([P, 2, 2 * P], F32, tag="turned")
+            for j in range(2):
+                t = 2 * half + j
+                for u in range(2):
+                    nc.tensor.transpose(
+                        out=turned[:, u, j * P : (j + 1) * P],
+                        in_=x_words[:, t, PASS_WORDS * g + u : PASS_WORDS * (g + 1) : 2],
+                        identity=ident[:],
                     )
-            nc.vector.quantize_mx(
-                out=codes[:].rearrange("p g n -> p (g n)").bitcast(FP8X4),
-                scales=scales[:].rearrange("p g n -> p (g n)"),
-                in_=grouped[:].rearrange("p g n -> p (g n)"),
+            grouped_words = grouped[c][:, g, :].bitcast(F32).rearrange("p (n u) -> p n u", u=2)
+            copy_out(
+                out=grouped_words[:, 2 * P * half : 2 * P * (half + 1), :],
+                in_=turned[:].rearrange("p u n -> p n u"),
             )
-            return codes, scales
 
-        def project(s, codes, scales):
-            y_cols = work.tile([P, 2, CHUNK], F32)
-            for h in range(2):
-                w = first_weight(s) + h
-                acc = acc_pool.tile([P, CHUNK], F32, tag="acc")
-                for g in range(PASSES):
-                    nc.tensor.matmul_mx(
-                        out=acc[:],
-                        lhsT=w_words[:, w, g, :].bitcast(FP8X4),
-                        lhsT_scale=w_scales[:, w, g, :],
-                        rhs=codes[:, g, :].bitcast(FP8X4),
-                        rhs_scale=scales[:, g, :],
-                        start=(g == 0),
-                        stop=(g == PASSES - 1),
-                    )
+        def quantise(c):
+            nc.vector.quantize_mx(
+                out=codes[c][:].rearrange("p g n -> p (g n)").bitcast(FP8X4),
+                scales=scales[c][:].rearrange("p g n -> p (g n)"),
+                in_=grouped[c][:].rearrange("p g n -> p (g n)"),
+            )
+
+        def project(c, h):
+            w = first_weight(c // BATCH) + h
+            if h == 0:
+                y_cols[c] = work.tile([P, 2, CHUNK], F32, name="y_cols")
+            acc = acc_pool.tile([P, CHUNK], F32, tag="acc")
+            for g in range(PASSES):
+                nc.tensor.matmul_mx(
+                    out=acc[:],
+                    lhsT=w_words[:, w, g, :].bitcast(FP8X4),
+                    lhsT_scale=w_scales[:, w, g, :],
+                    rhs=codes[c][:, g, :].bitcast(FP8X4),
+                    rhs_scale=scales[c][:, g, :],
+                    start=(g == 0),
+                    stop=(g == PASSES - 1),
+                )
+            nc.scalar.activation(
+                out=y_cols[c][:, h, :], in_=acc[:], func=ACT.Identity, bias=bias_col[:, w : w + 1], scale=1.0
+            )
+
+        def turn_back(c, h):
+            if h == 0:
+                sum_sq[c] = work.tile([P, 2, ROWS_PER_PART], F32, name="sum_sq")
+                inv_rms[c] = work.tile([P, 2, ROWS_PER_PART], F32, name="inv_rms")
+                squares[c] = work.tile([P, 2, ROWS_PER_PART, D], F32, name="squares")
+            y = back_pool.tile([P, ROWS_PER_PART, D], F32, tag="back", name="back")
+            ys[c, h] = y
+            for t in range(ROWS_PER_PART):
+                nc.tensor.transpose(out=y[:, t, :], in_=y_cols[c][:, h, t * P : (t + 1) * P], identity=ident[:])
+            for t in range(ROWS_PER_PART):
                 nc.scalar.activation(
-                    out=y_cols[:, h, :], in_=acc[:], func=ACT.Identity, bias=bias_col[:, w : w + 1], scale=1.0
-                )
-            return y_cols
-
-        def norm_rotate_store(s, b, y_cols, between, last_chunk):
-            sum_sq = work.tile([P, 2, ROWS_PER_PART], F32)
-            inv_rms = work.tile([P, 2, ROWS_PER_PART], F32)
-            squares = work.tile([P, 2, ROWS_PER_PART, D], F32)
-            products = work.tile([P, 2, ROWS_PER_PART, 2, D], F32)
-            result = out_pool.tile([P, 2, ROWS_PER_PART, D], F32)
-            ys = []
-            for h in range(2):
-                y = back_pool.tile([P, ROWS_PER_PART, D], F32)
-                ys.append(y)
-                for t in range(ROWS_PER_PART):
-                    nc.tensor.transpose(out=y[:, t, :], in_=y_cols[:, h, t * P : (t + 1) * P], identity=ident[:])
-                for t in range(ROWS_PER_PART):
-                    nc.scalar.activation(
-                        out=squares[:, h, t, :], in_=y[:, t, :], func=ACT.Square, accum_out=sum_sq[:, h, t : t + 1]
-                    )
-                nc.scalar.activation(
-                    out=inv_rms[:, h, :], in_=sum_sq[:, h, :], func=ACT.Abs_reciprocal_sqrt,
-                    bias=eps[:, 0:1], scale=1.0 / D,
-                )
-            between()
-            for h in range(2):
-                y = ys[h]
-                for t in range(ROWS_PER_PART):
-                    r = inv_rms[:, h, t : t + 1]
-                    nc.vector.scalar_tensor_tensor(
-                        out=products[:, h, t], in0=y[:, t, :].unsqueeze(1).to_broadcast([P, 2, D]), scalar=r,
-                        in1=tables[:, s, h, t], op0=ALU.mult, op1=ALU.mult,
-                    )
-                    first = {(0, ROWS_PER_PART - 1): 0, (1, 1): 0, (1, ROWS_PER_PART - 1): 2}.get((h, t))
-                    if first is not None:
-                        very_last = last_chunk and h == 1 and t == ROWS_PER_PART - 1
-                        adder = nc.vector if very_last else nc.gpsimd
-                        adder.tensor_tensor(
-                            out=pairs(result[:, h, first : t + 1]), in0=pairs(products[:, h, first : t + 1, 0, :]),
-                            in1=pairs(products[:, h, first : t + 1, 1, :])[:, :, :, ::-1], op=ALU.add,
-                        )
-                nc.sync.dma_start(
-                    out=outs[h][b, s * CHUNK : (s + 1) * CHUNK, 0, :].rearrange(
-                        "(p t) d -> p (t d)", t=ROWS_PER_PART
-                    ),
-                    in_=result[:, h].rearrange("p t d -> p (t d)"),
+                    out=squares[c][:, h, t, :], in_=y[:, t, :], func=ACT.Square, accum_out=sum_sq[c][:, h, t : t + 1]
                 )
 
-        quantised = {}
-        projected = {}
+        def norm(c, h):
+            nc.scalar.activation(
+                out=inv_rms[c][:, h, :], in_=sum_sq[c][:, h, :], func=ACT.Abs_reciprocal_sqrt,
+                bias=eps[:, 0:1], scale=1.0 / D,
+            )
+
+        def rotate_store(c, h):
+            s, b = divmod(c, BATCH)
+            if h == 0:
+                products[c] = work.tile([P, 2, ROWS_PER_PART, 2, D], F32, name="products")
+                result[c] = out_pool.tile([P, 2, ROWS_PER_PART, D], F32, name="result")
+            y = ys[c, h]
+            for t in range(ROWS_PER_PART):
+                r = inv_rms[c][:, h, t : t + 1]
+                nc.vector.scalar_tensor_tensor(
+                    out=products[c][:, h, t], in0=y[:, t, :].unsqueeze(1).to_broadcast([P, 2, D]), scalar=r,
+                    in1=tables[:, s, h, t], op0=ALU.mult, op1=ALU.mult,
+                )
+                first = ADD_FIRST.get((h, t))
+                if first is not None:
+                    very_last = c == N_CHUNKS - 1 and h == 1 and t == ROWS_PER_PART - 1
+                    adder = nc.vector if very_last else nc.gpsimd
+                    adder.tensor_tensor(
+                        out=pairs(result[c][:, h, first : t + 1]), in0=pairs(products[c][:, h, first : t + 1, 0, :]),
+                        in1=pairs(products[c][:, h, first : t + 1, 1, :])[:, :, :, ::-1], op=ALU.add,
+                    )
+            nc.sync.dma_start(
+                out=outs[h][b, s * CHUNK : (s + 1) * CHUNK, 0, :].rearrange("(p t) d -> p (t d)", t=ROWS_PER_PART),
+                in_=result[c][:, h].rearrange("p t d -> p (t d)"),
+            )
+
         with tc.manual_schedule():
             for c in range(N_CHUNKS + 2):
+                now, mid, old = c < N_CHUNKS, 1 <= c <= N_CHUNKS, c >= 2
                 if c + LOAD_AHEAD < N_CHUNKS:
                     x_tiles[c + LOAD_AHEAD] = load(c + LOAD_AHEAD)
-                if c + BATCH < N_CHUNKS:
-                    fill_table(c // BATCH + 1, c % BATCH)
-                if c < N_CHUNKS:
-                    quantised[c] = turn_and_quantise(x_tiles[c])
-                def project_last():
-                    if 1 <= c <= N_CHUNKS:
-                        projected[c - 1] = project((c - 1) // BATCH, quantised[c - 1][0], quantised[c - 1][1])
-
-                if c >= 2:
-                    s, b = divmod(c - 2, BATCH)
-                    norm_rotate_store(s, b, projected[c - 2], project_last, c - 2 == N_CHUNKS - 1)
-                else:
-                    project_last()
+                if c == 0:
+                    load_rotary(nc.sync, slice(1, SEQ_CHUNKS))
+                if old and c - 2 + BATCH < N_CHUNKS:
+                    fill_table((c - 2) // BATCH + 1, (c - 2) % BATCH)
+                banks = HALF_MAJOR if c == 0 else PASS_MAJOR
+                if now:
+                    open_chunk(c)
+                    turn(c, banks[0], nc.scalar.copy)
+                if old:
+                    turn_back(c - 2, 0)
+                if now:
+                    turn(c, banks[1], nc.scalar.copy)
+                if old:
+                    norm(c - 2, 0)
+                if now:
+                    turn(c, banks[2], nc.scalar.copy)
+                if c == 1:
+                    spread_biases_and_gains()
+                    for piece in range(TABLE_PIECES):
+                        fill_table(0, piece)
+                if now:
+                    turn(c, banks[3], nc.vector.tensor_copy)
+                if old:
+                    rotate_store(c - 2, 0)
+                if now:
+                    quantise(c)
+                if mid:
+                    project(c - 1, 0)
+                if old:
+                    turn_back(c - 2, 1)
+                if mid:
+                    project(c - 1, 1)
+                if old:
+                    norm(c - 2, 1)
+                    rotate_store(c - 2, 1)

@@ -31,10 +31,12 @@ LOAD_AHEAD = 3
 TABLE_PIECES = 4
 assert TABLE_PIECES == BATCH
 
-PASS_MAJOR = [(0, 0), (0, 1), (1, 0), (1, 1)]
-HALF_MAJOR = [(0, 0), (1, 0), (0, 1), (1, 1)]
-
-ADD_FIRST = {(0, 3): 0, (1, 1): 0, (1, 3): 2}
+IMAGE, TEXT = (0, 1), (2, 3)
+PIECE_BLOCKS = 2
+PIECE = PIECE_BLOCKS * P
+PIECES = ROWS_PER_PART // PIECE_BLOCKS
+N_PIECES = N_CHUNKS * PIECES
+MX_LAG, BACK_LAG = 2, 4
 
 FLOPS = 2 * BATCH * SEQ * K * 2 * D
 
@@ -76,13 +78,13 @@ def tile_fluxjointattention_pa_t_kernel(
     with ExitStack() as ctx:
         const = ctx.enter_context(tc.tile_pool(name="const", bufs=1))
         x_pool = ctx.enter_context(tc.tile_pool(name="x", bufs=LOAD_AHEAD + 1))
-        work = ctx.enter_context(tc.tile_pool(name="work", bufs=2))
+        work = ctx.enter_context(tc.tile_pool(name="work", bufs=3))
         out_pool = ctx.enter_context(tc.tile_pool(name="out", bufs=3))
-        turned_pool = ctx.enter_context(tc.psum_pool(name="turned", bufs=4))
+        turned_pool = ctx.enter_context(tc.psum_pool(name="turned", bufs=3))
         acc_pool = ctx.enter_context(tc.psum_pool(name="acc", bufs=2))
-        back_pool = ctx.enter_context(tc.psum_pool(name="back", bufs=2))
+        back_pool = ctx.enter_context(tc.psum_pool(name="back", bufs=3))
 
-        def load(c, pieces=1):
+        def load(c, pieces=1, between=None):
             s, b = divmod(c, BATCH)
             if s == 0:
                 rows = encoder_hidden_states[b]
@@ -93,6 +95,8 @@ def tile_fluxjointattention_pa_t_kernel(
             step = ROWS_PER_PART // pieces
             for t in range(0, ROWS_PER_PART, step):
                 nc.sync.dma_start(out=x_rows[:, t : t + step, :], in_=by_part[:, t : t + step, :])
+                if between and t == 0:
+                    between()
             return x_rows
 
         x_tiles = {}
@@ -132,25 +136,28 @@ def tile_fluxjointattention_pa_t_kernel(
         bias_rows32 = const.tile([P, P], F32)
         bias_col = const.tile([P, 4], F32)
 
-        for w in range(4):
-            nc.gpsimd.dma_start(
-                out=gain_row[0:1, w * D : (w + 1) * D], in_=gains[w].rearrange("(o d) -> o d", o=1)
-            )
+        for queue, pair in ((nc.sync, TEXT), (nc.scalar, IMAGE)):
+            for w in pair:
+                queue.dma_start(out=gain_row[0:1, w * D : (w + 1) * D], in_=gains[w].rearrange("(o d) -> o d", o=1))
         ones = const.tile([P, P], BF16)
         nc.vector.memset(ones[:], 1.0)
         gain_c = const.tile([P, 4, D], F32)
         gain_s = const.tile([P, 4, D], F32)
 
-        def spread_biases_and_gains():
+        def spread_biases():
             nc.gpsimd.tensor_copy(out=bias_rows32[:], in_=bias_rows[:])
             bias_turned = back_pool.tile([P, 4 * D], F32, tag="back")
             nc.tensor.transpose(out=bias_turned[:, 0:P], in_=bias_rows32[:], identity=ident[:])
-            gain_all = back_pool.tile([P, 4 * D], F32, tag="back")
-            nc.tensor.matmul(out=gain_all[:], lhsT=ones[:], rhs=gain_row[:], start=True, stop=True)
             nc.vector.tensor_copy(out=bias_col[:], in_=bias_turned[:, 0:4])
-            nc.vector.tensor_copy(out=gain_c[:].rearrange("p w d -> p (w d)"), in_=gain_all[:])
-            gain_pairs = gain_all[:].rearrange("p (w i e) -> p w i e", w=4, e=2)
-            gain_s_pairs = gain_s[:].rearrange("p w (i e) -> p w i e", e=2)
+
+        def spread_gains(pair):
+            cols = slice(pair[0] * D, (pair[1] + 1) * D)
+            ws = slice(pair[0], pair[1] + 1)
+            gain_all = back_pool.tile([P, 2 * D], F32, tag="back")
+            nc.tensor.matmul(out=gain_all[:], lhsT=ones[:], rhs=gain_row[:, cols], start=True, stop=True)
+            nc.vector.tensor_copy(out=gain_c[:, ws].rearrange("p w d -> p (w d)"), in_=gain_all[:])
+            gain_pairs = gain_all[:].rearrange("p (w i e) -> p w i e", w=2, e=2)
+            gain_s_pairs = gain_s[:, ws].rearrange("p w (i e) -> p w i e", e=2)
             nc.vector.tensor_copy(out=gain_s_pairs[:, :, :, 0], in_=gain_pairs[:, :, :, 0])
             nc.vector.tensor_scalar_mul(out=gain_s_pairs[:, :, :, 1], in0=gain_pairs[:, :, :, 1], scalar1=-1.0)
 
@@ -164,11 +171,13 @@ def tile_fluxjointattention_pa_t_kernel(
                     in_=table.rearrange("(s p t) d -> p s (t d)", s=SEQ_CHUNKS, t=ROWS_PER_PART)[:, part, :],
                 )
 
-        x_tiles[1] = load(1)
+        def first_weights():
+            load_weight(2)
+            load_weight(3)
+
+        x_tiles[1] = load(1, pieces=2, between=first_weights)
         load_rotary(nc.sync, slice(0, 1))
-        load_weight(2)
-        load_weight(3)
-        x_tiles[2] = load(2)
+        x_tiles[2] = load(2, pieces=2)
         load_weight(0)
         load_weight(1)
 
@@ -177,155 +186,165 @@ def tile_fluxjointattention_pa_t_kernel(
         def pairs(ap):
             return ap.rearrange("p t (i e) -> p t i e", e=2)
 
-        def fill_table(s, piece):
+        def fill_table(engine, s, piece, ts=slice(0, ROWS_PER_PART)):
             h, kind = divmod(piece, 2)
             w = first_weight(s) + h
             if kind == 0:
-                rows, gain = pairs(cos_rows[:, s]), gain_c
+                rows, gain = pairs(cos_rows[:, s, ts]), gain_c
             else:
-                rows, gain = pairs(sin_rows[:, s])[:, :, :, ::-1], gain_s
-            nc.gpsimd.tensor_tensor(
-                out=pairs(tables[:, s, h, :, kind, :]),
+                rows, gain = pairs(sin_rows[:, s, ts])[:, :, :, ::-1], gain_s
+            engine.tensor_tensor(
+                out=pairs(tables[:, s, h, ts, kind, :]),
                 in0=rows,
-                in1=pairs(gain[:, w].unsqueeze(1).to_broadcast([P, ROWS_PER_PART, D])),
+                in1=pairs(gain[:, w].unsqueeze(1).to_broadcast([P, ts.stop - ts.start, D])),
                 op=ALU.mult,
             )
 
 
         grouped, codes, scales = {}, {}, {}
-        y_cols, ys, sum_sq, inv_rms, squares, products, result = {}, {}, {}, {}, {}, {}, {}
+        y_cols, ys, sum_sq, inv_rms, products, result = {}, {}, {}, {}, {}, {}
 
-        def open_chunk(c):
-            grouped[c] = work.tile([P, PASSES, 4 * CHUNK], BF16, align_bytes=64, name="grouped")
-            codes[c] = work.tile([P, PASSES, CHUNK], U32, align_bytes=64, name="codes")
-            scales[c] = work.tile([P, PASSES, CHUNK], U8, align_bytes=64, name="scales")
+        def open_piece(i):
+            grouped[i] = work.tile([P, PASSES, 4 * PIECE], BF16, align_bytes=64, name="grouped")
+            codes[i] = work.tile([P, PASSES, PIECE], U32, align_bytes=64, name="codes")
+            scales[i] = work.tile([P, PASSES, PIECE], U8, align_bytes=64, name="scales")
 
-        def turn(c, bank, copy_out):
-            g, half = bank
-            x_words = x_tiles[c][:].bitcast(F32)
-            turned = turned_pool.tile([P, 2, 2 * P], F32, tag="turned")
-            for j in range(2):
-                t = 2 * half + j
+        def turn(i, g, copy_out):
+            x_words = x_tiles[i // PIECES][:].bitcast(F32)
+            turned = turned_pool.tile([P, 2, PIECE], F32, tag="turned")
+            for j in range(PIECE_BLOCKS):
+                t = PIECE_BLOCKS * (i % PIECES) + j
                 for u in range(2):
                     nc.tensor.transpose(
                         out=turned[:, u, j * P : (j + 1) * P],
                         in_=x_words[:, t, PASS_WORDS * g + u : PASS_WORDS * (g + 1) : 2],
                         identity=ident[:],
                     )
-            grouped_words = grouped[c][:, g, :].bitcast(F32).rearrange("p (n u) -> p n u", u=2)
             copy_out(
-                out=grouped_words[:, 2 * P * half : 2 * P * (half + 1), :],
+                out=grouped[i][:, g, :].bitcast(F32).rearrange("p (n u) -> p n u", u=2),
                 in_=turned[:].rearrange("p u n -> p n u"),
             )
 
-        def quantise(c):
+        def quantise(i):
             nc.vector.quantize_mx(
-                out=codes[c][:].rearrange("p g n -> p (g n)").bitcast(FP8X4),
-                scales=scales[c][:].rearrange("p g n -> p (g n)"),
-                in_=grouped[c][:].rearrange("p g n -> p (g n)"),
+                out=codes[i][:].rearrange("p g n -> p (g n)").bitcast(FP8X4),
+                scales=scales[i][:].rearrange("p g n -> p (g n)"),
+                in_=grouped[i][:].rearrange("p g n -> p (g n)"),
             )
 
-        def project(c, h):
-            w = first_weight(c // BATCH) + h
-            if h == 0:
-                y_cols[c] = work.tile([P, 2, CHUNK], F32, name="y_cols")
-            acc = acc_pool.tile([P, CHUNK], F32, tag="acc")
-            for g in range(PASSES):
-                nc.tensor.matmul_mx(
-                    out=acc[:],
-                    lhsT=w_words[:, w, g, :].bitcast(FP8X4),
-                    lhsT_scale=w_scales[:, w, g, :],
-                    rhs=codes[c][:, g, :].bitcast(FP8X4),
-                    rhs_scale=scales[c][:, g, :],
-                    start=(g == 0),
-                    stop=(g == PASSES - 1),
-                )
-            nc.scalar.activation(
-                out=y_cols[c][:, h, :], in_=acc[:], func=ACT.Identity, bias=bias_col[:, w : w + 1], scale=1.0
-            )
-
-        def turn_back(c, h):
-            if h == 0:
-                sum_sq[c] = work.tile([P, 2, ROWS_PER_PART], F32, name="sum_sq")
-                inv_rms[c] = work.tile([P, 2, ROWS_PER_PART], F32, name="inv_rms")
-                squares[c] = work.tile([P, 2, ROWS_PER_PART, D], F32, name="squares")
-            y = back_pool.tile([P, ROWS_PER_PART, D], F32, tag="back", name="back")
-            ys[c, h] = y
-            for t in range(ROWS_PER_PART):
-                nc.tensor.transpose(out=y[:, t, :], in_=y_cols[c][:, h, t * P : (t + 1) * P], identity=ident[:])
-            for t in range(ROWS_PER_PART):
-                nc.scalar.activation(
-                    out=squares[c][:, h, t, :], in_=y[:, t, :], func=ACT.Square, accum_out=sum_sq[c][:, h, t : t + 1]
-                )
-
-        def norm(c, h):
-            nc.scalar.activation(
-                out=inv_rms[c][:, h, :], in_=sum_sq[c][:, h, :], func=ACT.Abs_reciprocal_sqrt,
-                bias=eps[:, 0:1], scale=1.0 / D,
-            )
-
-        def rotate_store(c, h):
-            s, b = divmod(c, BATCH)
-            if h == 0:
-                products[c] = work.tile([P, 2, ROWS_PER_PART, 2, D], F32, name="products")
-                result[c] = out_pool.tile([P, 2, ROWS_PER_PART, D], F32, name="result")
-            y = ys[c, h]
-            for t in range(ROWS_PER_PART):
-                r = inv_rms[c][:, h, t : t + 1]
-                nc.vector.scalar_tensor_tensor(
-                    out=products[c][:, h, t], in0=y[:, t, :].unsqueeze(1).to_broadcast([P, 2, D]), scalar=r,
-                    in1=tables[:, s, h, t], op0=ALU.mult, op1=ALU.mult,
-                )
-                first = ADD_FIRST.get((h, t))
-                if first is not None:
-                    very_last = c == N_CHUNKS - 1 and h == 1 and t == ROWS_PER_PART - 1
-                    adder = nc.vector if very_last else nc.gpsimd
-                    adder.tensor_tensor(
-                        out=pairs(result[c][:, h, first : t + 1]), in0=pairs(products[c][:, h, first : t + 1, 0, :]),
-                        in1=pairs(products[c][:, h, first : t + 1, 1, :])[:, :, :, ::-1], op=ALU.add,
+        def project(i):
+            y_cols[i] = work.tile([P, 2, PIECE], F32, name="y_cols")
+            acc = acc_pool.tile([P, 2, PIECE], F32, tag="acc")
+            for h in range(2):
+                w = first_weight(i // PIECES // BATCH) + h
+                for g in range(PASSES):
+                    nc.tensor.matmul_mx(
+                        out=acc[:, h, :],
+                        lhsT=w_words[:, w, g, :].bitcast(FP8X4),
+                        lhsT_scale=w_scales[:, w, g, :],
+                        rhs=codes[i][:, g, :].bitcast(FP8X4),
+                        rhs_scale=scales[i][:, g, :],
+                        start=(g == 0),
+                        stop=(g == PASSES - 1),
                     )
-            nc.sync.dma_start(
-                out=outs[h][b, s * CHUNK : (s + 1) * CHUNK, 0, :].rearrange("(p t) d -> p (t d)", t=ROWS_PER_PART),
-                in_=result[c][:, h].rearrange("p t d -> p (t d)"),
+            for h in range(2):
+                w = first_weight(i // PIECES // BATCH) + h
+                nc.scalar.activation(
+                    out=y_cols[i][:, h, :], in_=acc[:, h, :], func=ACT.Identity, bias=bias_col[:, w : w + 1], scale=1.0
+                )
+
+        def turn_back(i):
+            sum_sq[i] = work.tile([P, 2, PIECE_BLOCKS], F32, name="sum_sq")
+            squares = work.tile([P, 2, PIECE_BLOCKS, D], F32, name="squares")
+            y = back_pool.tile([P, 2, PIECE_BLOCKS, D], F32, tag="back", name="back")
+            ys[i] = y
+            for h in range(2):
+                for j in range(PIECE_BLOCKS):
+                    nc.tensor.transpose(
+                        out=y[:, h, j, :], in_=y_cols[i][:, h, j * P : (j + 1) * P], identity=ident[:]
+                    )
+            for h in range(2):
+                for j in range(PIECE_BLOCKS):
+                    nc.scalar.activation(
+                        out=squares[:, h, j, :], in_=y[:, h, j, :], func=ACT.Square, accum_out=sum_sq[i][:, h, j : j + 1]
+                    )
+
+        def norm(i):
+            inv_rms[i] = work.tile([P, 2, PIECE_BLOCKS], F32, name="inv_rms")
+            nc.scalar.activation(
+                out=inv_rms[i][:].rearrange("p h j -> p (h j)"), in_=sum_sq[i][:].rearrange("p h j -> p (h j)"),
+                func=ACT.Abs_reciprocal_sqrt, bias=eps[:, 0:1], scale=1.0 / D,
             )
+
+        def rotate_store(i):
+            c, half = divmod(i, PIECES)
+            s, b = divmod(c, BATCH)
+            products = work.tile([P, 2, PIECE_BLOCKS, 2, D], F32, name="products")
+            if half == 0:
+                result[c] = out_pool.tile([P, PIECES, 2, PIECE_BLOCKS, D], F32, name="result")
+            last = i == N_PIECES - 1
+
+            def add(engine, heads):
+                flat = products[:, heads].rearrange("p h j k d -> p (h j) k d")
+                engine.tensor_tensor(
+                    out=pairs(result[c][:, half, heads].rearrange("p h j d -> p (h j) d")),
+                    in0=pairs(flat[:, :, 0, :]), in1=pairs(flat[:, :, 1, :])[:, :, :, ::-1], op=ALU.add,
+                )
+
+            for h in range(2):
+                for j in range(PIECE_BLOCKS):
+                    nc.vector.scalar_tensor_tensor(
+                        out=products[:, h, j], in0=ys[i][:, h, j, :].unsqueeze(1).to_broadcast([P, 2, D]),
+                        scalar=inv_rms[i][:, h, j : j + 1], in1=tables[:, s, h, PIECE_BLOCKS * half + j],
+                        op0=ALU.mult, op1=ALU.mult,
+                    )
+                if last:
+                    add(nc.gpsimd if h == 0 else nc.vector, slice(h, h + 1))
+            if not last:
+                add(nc.gpsimd, slice(0, 2))
+            stored = slice(half, half + 1) if c == N_CHUNKS - 1 else slice(0, PIECES)
+            if stored.stop == half + 1:
+                for h in range(2):
+                    nc.sync.dma_start(
+                        out=outs[h][b, s * CHUNK : (s + 1) * CHUNK, 0, :].rearrange(
+                            "(p f j) d -> p f (j d)", f=PIECES, j=PIECE_BLOCKS
+                        )[:, stored, :],
+                        in_=result[c][:, stored, h].rearrange("p f j d -> p f (j d)"),
+                    )
 
         with tc.manual_schedule():
-            for c in range(N_CHUNKS + 2):
-                now, mid, old = c < N_CHUNKS, 1 <= c <= N_CHUNKS, c >= 2
-                if c + LOAD_AHEAD < N_CHUNKS:
-                    x_tiles[c + LOAD_AHEAD] = load(c + LOAD_AHEAD)
-                if c == 0:
-                    load_rotary(nc.sync, slice(1, SEQ_CHUNKS))
-                if old and c - 2 + BATCH < N_CHUNKS:
-                    fill_table((c - 2) // BATCH + 1, (c - 2) % BATCH)
-                banks = HALF_MAJOR if c == 0 else PASS_MAJOR
-                if now:
-                    open_chunk(c)
-                    turn(c, banks[0], nc.scalar.copy)
+            for i in range(N_PIECES + BACK_LAG):
+                c, half = divmod(i, PIECES)
+                now, mid, old = i < N_PIECES, 0 <= i - MX_LAG < N_PIECES, i >= BACK_LAG
+                if half == 0:
+                    if c + LOAD_AHEAD < N_CHUNKS:
+                        x_tiles[c + LOAD_AHEAD] = load(c + LOAD_AHEAD)
+                    if c == 0:
+                        load_rotary(nc.sync, slice(1, SEQ_CHUNKS))
+                    if c >= 2 and c - 2 + BATCH < N_CHUNKS:
+                        fill_table(nc.gpsimd, (c - 2) // BATCH + 1, (c - 2) % BATCH)
                 if old:
-                    turn_back(c - 2, 0)
+                    turn_back(i - BACK_LAG)
                 if now:
-                    turn(c, banks[1], nc.scalar.copy)
+                    open_piece(i)
+                    turn(i, half, nc.scalar.copy)
                 if old:
-                    norm(c - 2, 0)
+                    norm(i - BACK_LAG)
+                if i == MX_LAG:
+                    spread_biases()
+                if mid:
+                    project(i - MX_LAG)
                 if now:
-                    turn(c, banks[2], nc.scalar.copy)
-                if c == 1:
-                    spread_biases_and_gains()
+                    turn(i, 1 - half, nc.vector.tensor_copy if half == 0 else nc.scalar.copy)
+                if i == MX_LAG:
+                    spread_gains(TEXT)
+                if old:
+                    rotate_store(i - BACK_LAG)
+                if i == MX_LAG + 1:
+                    spread_gains(IMAGE)
+                if now:
+                    quantise(i)
+                if 0 <= i - MX_LAG < PIECES:
+                    ts = slice(PIECE_BLOCKS * (i - MX_LAG), PIECE_BLOCKS * (i - MX_LAG + 1))
                     for piece in range(TABLE_PIECES):
-                        fill_table(0, piece)
-                if now:
-                    turn(c, banks[3], nc.vector.tensor_copy)
-                if old:
-                    rotate_store(c - 2, 0)
-                if now:
-                    quantise(c)
-                if mid:
-                    project(c - 1, 0)
-                if old:
-                    turn_back(c - 2, 1)
-                if mid:
-                    project(c - 1, 1)
-                if old:
-                    norm(c - 2, 1)
-                    rotate_store(c - 2, 1)
+                        fill_table(nc.vector, 0, piece, ts)

@@ -36,7 +36,7 @@ PIECE_BLOCKS = 2
 PIECE = PIECE_BLOCKS * P
 PIECES = ROWS_PER_PART // PIECE_BLOCKS
 N_PIECES = N_CHUNKS * PIECES
-MX_LAG, BACK_LAG = 2, 4
+MX_LAG, BACK_LAG = 3, 5
 
 FLOPS = 2 * BATCH * SEQ * K * 2 * D
 
@@ -78,13 +78,13 @@ def tile_fluxjointattention_pa_t_kernel(
     with ExitStack() as ctx:
         const = ctx.enter_context(tc.tile_pool(name="const", bufs=1))
         x_pool = ctx.enter_context(tc.tile_pool(name="x", bufs=LOAD_AHEAD + 1))
-        work = ctx.enter_context(tc.tile_pool(name="work", bufs=3))
+        work = ctx.enter_context(tc.tile_pool(name="work", bufs=4))
         out_pool = ctx.enter_context(tc.tile_pool(name="out", bufs=3))
         turned_pool = ctx.enter_context(tc.psum_pool(name="turned", bufs=3))
         acc_pool = ctx.enter_context(tc.psum_pool(name="acc", bufs=2))
         back_pool = ctx.enter_context(tc.psum_pool(name="back", bufs=3))
 
-        def load(c, pieces=1, between=None):
+        def load(c, pieces=1):
             s, b = divmod(c, BATCH)
             if s == 0:
                 rows = encoder_hidden_states[b]
@@ -95,8 +95,6 @@ def tile_fluxjointattention_pa_t_kernel(
             step = ROWS_PER_PART // pieces
             for t in range(0, ROWS_PER_PART, step):
                 nc.sync.dma_start(out=x_rows[:, t : t + step, :], in_=by_part[:, t : t + step, :])
-                if between and t == 0:
-                    between()
             return x_rows
 
         x_tiles = {}
@@ -171,13 +169,12 @@ def tile_fluxjointattention_pa_t_kernel(
                     in_=table.rearrange("(s p t) d -> p s (t d)", s=SEQ_CHUNKS, t=ROWS_PER_PART)[:, part, :],
                 )
 
-        def first_weights():
-            load_weight(2)
-            load_weight(3)
-
-        x_tiles[1] = load(1, pieces=2, between=first_weights)
+        x_tiles[1] = load(1, pieces=2)
         load_rotary(nc.sync, slice(0, 1))
+        load_weight(2)
+        load_weight(3)
         x_tiles[2] = load(2, pieces=2)
+        x_tiles[3] = load(3)
         load_weight(0)
         load_weight(1)
 
@@ -317,7 +314,7 @@ def tile_fluxjointattention_pa_t_kernel(
                 c, half = divmod(i, PIECES)
                 now, mid, old = i < N_PIECES, 0 <= i - MX_LAG < N_PIECES, i >= BACK_LAG
                 if half == 0:
-                    if c + LOAD_AHEAD < N_CHUNKS:
+                    if 1 <= c and c + LOAD_AHEAD < N_CHUNKS:
                         x_tiles[c + LOAD_AHEAD] = load(c + LOAD_AHEAD)
                     if c == 0:
                         load_rotary(nc.sync, slice(1, SEQ_CHUNKS))
@@ -330,21 +327,21 @@ def tile_fluxjointattention_pa_t_kernel(
                     turn(i, half, nc.scalar.copy)
                 if old:
                     norm(i - BACK_LAG)
-                if i == MX_LAG:
+                if i == 2:
                     spread_biases()
                 if mid:
                     project(i - MX_LAG)
                 if now:
                     turn(i, 1 - half, nc.vector.tensor_copy if half == 0 else nc.scalar.copy)
-                if i == MX_LAG:
+                if i == 2:
                     spread_gains(TEXT)
                 if old:
                     rotate_store(i - BACK_LAG)
-                if i == MX_LAG + 1:
+                if i == 3:
                     spread_gains(IMAGE)
                 if now:
                     quantise(i)
-                if 0 <= i - MX_LAG < PIECES:
-                    ts = slice(PIECE_BLOCKS * (i - MX_LAG), PIECE_BLOCKS * (i - MX_LAG + 1))
+                if 2 <= i < 2 + PIECES:
+                    ts = slice(PIECE_BLOCKS * (i - 2), PIECE_BLOCKS * (i - 1))
                     for piece in range(TABLE_PIECES):
                         fill_table(nc.vector, 0, piece, ts)

@@ -36,6 +36,7 @@ PIECE_BLOCKS = 2
 PIECE = PIECE_BLOCKS * P
 PIECES = ROWS_PER_PART // PIECE_BLOCKS
 N_PIECES = N_CHUNKS * PIECES
+VECTOR_COPIES = (0, 2)
 MX_LAG, BACK_LAG = 3, 5
 
 FLOPS = 2 * BATCH * SEQ * K * 2 * D
@@ -78,7 +79,8 @@ def tile_fluxjointattention_pa_t_kernel(
     with ExitStack() as ctx:
         const = ctx.enter_context(tc.tile_pool(name="const", bufs=1))
         x_pool = ctx.enter_context(tc.tile_pool(name="x", bufs=LOAD_AHEAD + 1))
-        work = ctx.enter_context(tc.tile_pool(name="work", bufs=4))
+        work = ctx.enter_context(tc.tile_pool(name="work", bufs=5))
+        product_pool = ctx.enter_context(tc.tile_pool(name="products", bufs=6))
         out_pool = ctx.enter_context(tc.tile_pool(name="out", bufs=3))
         turned_pool = ctx.enter_context(tc.psum_pool(name="turned", bufs=3))
         acc_pool = ctx.enter_context(tc.psum_pool(name="acc", bufs=2))
@@ -170,11 +172,13 @@ def tile_fluxjointattention_pa_t_kernel(
                 )
 
         x_tiles[1] = load(1, pieces=2)
-        load_rotary(nc.sync, slice(0, 1))
+        load_rotary(nc.sync, slice(0, 2))
         load_weight(2)
         load_weight(3)
+        load_rotary(nc.sync, slice(2, 3))
         x_tiles[2] = load(2, pieces=2)
         x_tiles[3] = load(3)
+        load_rotary(nc.sync, slice(3, 4))
         load_weight(0)
         load_weight(1)
 
@@ -276,7 +280,7 @@ def tile_fluxjointattention_pa_t_kernel(
         def rotate_store(i):
             c, half = divmod(i, PIECES)
             s, b = divmod(c, BATCH)
-            products = work.tile([P, 2, PIECE_BLOCKS, 2, D], F32, name="products")
+            products = product_pool.tile([P, 2, PIECE_BLOCKS, 2, D], F32, name="products")
             if half == 0:
                 result[c] = out_pool.tile([P, PIECES, 2, PIECE_BLOCKS, D], F32, name="result")
             last = i == N_PIECES - 1
@@ -316,29 +320,26 @@ def tile_fluxjointattention_pa_t_kernel(
                 if half == 0:
                     if 1 <= c and c + LOAD_AHEAD < N_CHUNKS:
                         x_tiles[c + LOAD_AHEAD] = load(c + LOAD_AHEAD)
-                    if c == 0:
-                        load_rotary(nc.sync, slice(1, SEQ_CHUNKS))
                     if c >= 2 and c - 2 + BATCH < N_CHUNKS:
                         fill_table(nc.gpsimd, (c - 2) // BATCH + 1, (c - 2) % BATCH)
                 if old:
                     turn_back(i - BACK_LAG)
-                if now:
-                    open_piece(i)
-                    turn(i, half, nc.scalar.copy)
-                if old:
-                    norm(i - BACK_LAG)
-                if i == 2:
-                    spread_biases()
                 if mid:
                     project(i - MX_LAG)
+                if old:
+                    norm(i - BACK_LAG)
                 if now:
-                    turn(i, 1 - half, nc.vector.tensor_copy if half == 0 else nc.scalar.copy)
+                    open_piece(i)
+                    turn(i, 0, nc.scalar.copy)
+                if i == 2:
+                    spread_biases()
+                if now:
+                    turn(i, 1, nc.vector.tensor_copy if i % 6 in VECTOR_COPIES else nc.scalar.copy)
                 if i == 2:
                     spread_gains(TEXT)
+                    spread_gains(IMAGE)
                 if old:
                     rotate_store(i - BACK_LAG)
-                if i == 3:
-                    spread_gains(IMAGE)
                 if now:
                     quantise(i)
                 if 2 <= i < 2 + PIECES:

@@ -172,15 +172,11 @@ def tile_fluxjointattention_pa_t_kernel(
                 )
 
         x_tiles[1] = load(1, pieces=2)
-        load_rotary(nc.sync, slice(0, 2))
         load_weight(2)
         load_weight(3)
-        load_rotary(nc.sync, slice(2, 3))
         x_tiles[2] = load(2, pieces=2)
+        load_rotary(nc.sync, slice(0, 2))
         x_tiles[3] = load(3)
-        load_rotary(nc.sync, slice(3, 4))
-        load_weight(0)
-        load_weight(1)
 
         tables = const.tile([P, SEQ_CHUNKS, 2, ROWS_PER_PART, 2, D], F32)
 
@@ -320,11 +316,16 @@ def tile_fluxjointattention_pa_t_kernel(
                 if half == 0:
                     if 1 <= c and c + LOAD_AHEAD < N_CHUNKS:
                         x_tiles[c + LOAD_AHEAD] = load(c + LOAD_AHEAD)
+                    if c == 1:
+                        load_weight(0)
+                        load_weight(1)
+                    if c in (2, 3):
+                        load_rotary(nc.sync, slice(c, c + 1))
                     if c >= 2 and c - 2 + BATCH < N_CHUNKS:
                         fill_table(nc.gpsimd, (c - 2) // BATCH + 1, (c - 2) % BATCH)
                 if old:
                     turn_back(i - BACK_LAG)
-                if mid:
+                if mid and i > MX_LAG:
                     project(i - MX_LAG)
                 if old:
                     norm(i - BACK_LAG)
@@ -335,14 +336,16 @@ def tile_fluxjointattention_pa_t_kernel(
                     spread_biases()
                 if now:
                     turn(i, 1, nc.vector.tensor_copy if i % 6 in VECTOR_COPIES else nc.scalar.copy)
-                if i == 2:
+                if i == MX_LAG:
+                    project(0)
+                if i == 3:
                     spread_gains(TEXT)
                     spread_gains(IMAGE)
                 if old:
                     rotate_store(i - BACK_LAG)
                 if now:
                     quantise(i)
-                if 2 <= i < 2 + PIECES:
-                    ts = slice(PIECE_BLOCKS * (i - 2), PIECE_BLOCKS * (i - 1))
+                if 3 <= i < 3 + PIECES:
+                    ts = slice(PIECE_BLOCKS * (i - 3), PIECE_BLOCKS * (i - 2))
                     for piece in range(TABLE_PIECES):
                         fill_table(nc.vector, 0, piece, ts)

from contextlib import ExitStack

import concourse.mybir as mybir
from concourse.masks import make_identity

F32 = mybir.dt.float32
BF16 = mybir.dt.bfloat16
I32 = mybir.dt.int32
U32 = mybir.dt.uint32
U8 = mybir.dt.uint8
FP8X4 = mybir.dt.float8_e4m3fn_x4
ACT = mybir.ActivationFunctionType
ALU = mybir.AluOpType

P = 128
BATCH = 4
TEXT_ROWS = 512
SEQ = 2048
K = 1024
D = 128
EPS = 1e-6

K_PASS = 4 * P
PASSES = K // K_PASS
PASS_WORDS = K_PASS // 2
ROWS_PER_PART = 4
CHUNK = P * ROWS_PER_PART
SEQ_CHUNKS = SEQ // CHUNK
N_CHUNKS = BATCH * SEQ_CHUNKS
LOAD_AHEAD = 3
TABLE_PIECES = 4
assert TABLE_PIECES == BATCH

IMAGE, TEXT = (0, 1), (2, 3)
PIECE_BLOCKS = 2
PIECE = PIECE_BLOCKS * P
PIECES = ROWS_PER_PART // PIECE_BLOCKS
N_PIECES = N_CHUNKS * PIECES
VECTOR_COPIES = (0, 2)
MX_LAG, BACK_LAG = 3, 5

FLOPS = 2 * BATCH * SEQ * K * 2 * D


def tile_fluxjointattention_pa_t_kernel(
    tc,
    hidden_states,
    encoder_hidden_states,
    rope_cos,
    rope_sin,
    Wq_words,
    Wq_scales,
    Wk_words,
    Wk_scales,
    Waq_words,
    Waq_scales,
    Wak_words,
    Wak_scales,
    bq,
    bk,
    baq,
    bak,
    g_q,
    g_k,
    g_aq,
    g_ak,
    out_0,
    out_1,
):
    nc = tc.nc
    weights = [(Wq_words, Wq_scales), (Wk_words, Wk_scales), (Waq_words, Waq_scales), (Wak_words, Wak_scales)]
    biases = [bq, bk, baq, bak]
    gains = [g_q, g_k, g_aq, g_ak]
    outs = [out_0, out_1]

    def first_weight(s):
        return 2 if s == 0 else 0

    with ExitStack() as ctx:
        const = ctx.enter_context(tc.tile_pool(name="const", bufs=1))
        x_pool = ctx.enter_context(tc.tile_pool(name="x", bufs=LOAD_AHEAD + 1))
        work = ctx.enter_context(tc.tile_pool(name="work", bufs=5))
        product_pool = ctx.enter_context(tc.tile_pool(name="products", bufs=6))
        out_pool = ctx.enter_context(tc.tile_pool(name="out", bufs=3))
        turned_pool = ctx.enter_context(tc.psum_pool(name="turned", bufs=3))
        acc_pool = ctx.enter_context(tc.psum_pool(name="acc", bufs=2))
        back_pool = ctx.enter_context(tc.psum_pool(name="back", bufs=3))

        def load(c, pieces=1):
            s, b = divmod(c, BATCH)
            if s == 0:
                rows = encoder_hidden_states[b]
            else:
                rows = hidden_states[b, (s - 1) * CHUNK : s * CHUNK, :]
            x_rows = x_pool.tile([P, ROWS_PER_PART, K], BF16)
            by_part = rows.rearrange("(p t) k -> p t k", t=ROWS_PER_PART)
            step = ROWS_PER_PART // pieces
            for t in range(0, ROWS_PER_PART, step):
                nc.sync.dma_start(out=x_rows[:, t : t + step, :], in_=by_part[:, t : t + step, :])
            return x_rows

        x_tiles = {}
        x_tiles[0] = load(0, pieces=2)

        bias_rows = const.tile([P, P], BF16)
        nc.vector.memset(bias_rows[:], 0.0)
        gain_row = const.tile([P, 4 * D], BF16)
        nc.vector.memset(gain_row[:], 0.0)
        eps = const.tile([P, 1], F32)
        nc.vector.memset(eps[:], EPS)

        ident = const.tile([P, P], F32)
        make_identity(nc, ident[:])

        w_words = const.tile([P, 4, PASSES, D], U32, align_bytes=64)
        w_scales = const.tile([P, 4, PASSES, D], U8, align_bytes=64)
        nc.vector.memset(w_scales[:].bitcast(I32), 0)

        def load_weight(w):
            words, scales = weights[w]
            nc.sync.dma_start(
                out=w_words[:, w].bitcast(I32),
                in_=words.rearrange("g p n t -> p g (n t)").bitcast(I32),
            )
            scale_rows = scales.rearrange("g (q r) n -> q r g n", r=4)
            for q in range(4):
                nc.sync.dma_start(
                    out=w_scales[32 * q : 32 * q + 4, w].bitcast(I32),
                    in_=scale_rows[q].bitcast(I32),
                )

        for w in range(4):
            nc.scalar.dma_start(out=bias_rows[w : w + 1, :], in_=biases[w].rearrange("(o d) -> o d", o=1))
        warm = const.tile([P, 1], F32)
        nc.scalar.activation(out=warm[:], in_=eps[:], func=ACT.Abs_reciprocal_sqrt)
        bias_rows32 = const.tile([P, P], F32)
        bias_col = const.tile([P, 4], F32)

        for queue, pair in ((nc.sync, TEXT), (nc.scalar, IMAGE)):
            for w in pair:
                queue.dma_start(out=gain_row[0:1, w * D : (w + 1) * D], in_=gains[w].rearrange("(o d) -> o d", o=1))
        ones = const.tile([P, P], BF16)
        nc.vector.memset(ones[:], 1.0)
        gain_c = const.tile([P, 4, D], F32)
        gain_s = const.tile([P, 4, D], F32)

        def spread_biases():
            nc.gpsimd.tensor_copy(out=bias_rows32[:], in_=bias_rows[:])
            bias_turned = back_pool.tile([P, 4 * D], F32, tag="back")
            nc.tensor.transpose(out=bias_turned[:, 0:P], in_=bias_rows32[:], identity=ident[:])
            nc.vector.tensor_copy(out=bias_col[:], in_=bias_turned[:, 0:4])

        def spread_gains(pair):
            cols = slice(pair[0] * D, (pair[1] + 1) * D)
            ws = slice(pair[0], pair[1] + 1)
            gain_all = back_pool.tile([P, 2 * D], F32, tag="back")
            nc.tensor.matmul(out=gain_all[:], lhsT=ones[:], rhs=gain_row[:, cols], start=True, stop=True)
            nc.vector.tensor_copy(out=gain_c[:, ws].rearrange("p w d -> p (w d)"), in_=gain_all[:])
            gain_pairs = gain_all[:].rearrange("p (w i e) -> p w i e", w=2, e=2)
            gain_s_pairs = gain_s[:, ws].rearrange("p w (i e) -> p w i e", e=2)
            nc.vector.tensor_copy(out=gain_s_pairs[:, :, :, 0], in_=gain_pairs[:, :, :, 0])
            nc.vector.tensor_scalar_mul(out=gain_s_pairs[:, :, :, 1], in0=gain_pairs[:, :, :, 1], scalar1=-1.0)

        cos_rows = const.tile([P, SEQ_CHUNKS, ROWS_PER_PART, D], BF16)
        sin_rows = const.tile([P, SEQ_CHUNKS, ROWS_PER_PART, D], BF16)

        def load_rotary(queue, part):
            for rows, table in ((cos_rows, rope_cos), (sin_rows, rope_sin)):
                queue.dma_start(
                    out=rows[:, part].rearrange("p s t d -> p s (t d)"),
                    in_=table.rearrange("(s p t) d -> p s (t d)", s=SEQ_CHUNKS, t=ROWS_PER_PART)[:, part, :],
                )

        x_tiles[1] = load(1, pieces=2)
        load_weight(2)
        load_weight(3)
        x_tiles[2] = load(2, pieces=2)
        load_rotary(nc.sync, slice(0, 2))
        x_tiles[3] = load(3)

        tables = const.tile([P, SEQ_CHUNKS, 2, ROWS_PER_PART, 2, D], F32)

        def pairs(ap):
            return ap.rearrange("p t (i e) -> p t i e", e=2)

        def fill_table(engine, s, piece, ts=slice(0, ROWS_PER_PART)):
            h, kind = divmod(piece, 2)
            w = first_weight(s) + h
            if kind == 0:
                rows, gain = pairs(cos_rows[:, s, ts]), gain_c
            else:
                rows, gain = pairs(sin_rows[:, s, ts])[:, :, :, ::-1], gain_s
            engine.tensor_tensor(
                out=pairs(tables[:, s, h, ts, kind, :]),
                in0=rows,
                in1=pairs(gain[:, w].unsqueeze(1).to_broadcast([P, ts.stop - ts.start, D])),
                op=ALU.mult,
            )


        grouped, codes, scales = {}, {}, {}
        y_cols, ys, sum_sq, inv_rms, products, result = {}, {}, {}, {}, {}, {}

        def open_piece(i):
            grouped[i] = work.tile([P, PASSES, 4 * PIECE], BF16, align_bytes=64, name="grouped")
            codes[i] = work.tile([P, PASSES, PIECE], U32, align_bytes=64, name="codes")
            scales[i] = work.tile([P, PASSES, PIECE], U8, align_bytes=64, name="scales")

        def turn(i, g, copy_out):
            x_words = x_tiles[i // PIECES][:].bitcast(F32)
            turned = turned_pool.tile([P, 2, PIECE], F32, tag="turned")
            for j in range(PIECE_BLOCKS):
                t = PIECE_BLOCKS * (i % PIECES) + j
                for u in range(2):
                    nc.tensor.transpose(
                        out=turned[:, u, j * P : (j + 1) * P],
                        in_=x_words[:, t, PASS_WORDS * g + u : PASS_WORDS * (g + 1) : 2],
                        identity=ident[:],
                    )
            copy_out(
                out=grouped[i][:, g, :].bitcast(F32).rearrange("p (n u) -> p n u", u=2),
                in_=turned[:].rearrange("p u n -> p n u"),
            )

        def quantise(i):
            nc.vector.quantize_mx(
                out=codes[i][:].rearrange("p g n -> p (g n)").bitcast(FP8X4),
                scales=scales[i][:].rearrange("p g n -> p (g n)"),
                in_=grouped[i][:].rearrange("p g n -> p (g n)"),
            )

        def project(i):
            y_cols[i] = work.tile([P, 2, PIECE], F32, name="y_cols")
            acc = acc_pool.tile([P, 2, PIECE], F32, tag="acc")
            for h in range(2):
                w = first_weight(i // PIECES // BATCH) + h
                for g in range(PASSES):
                    nc.tensor.matmul_mx(
                        out=acc[:, h, :],
                        lhsT=w_words[:, w, g, :].bitcast(FP8X4),
                        lhsT_scale=w_scales[:, w, g, :],
                        rhs=codes[i][:, g, :].bitcast(FP8X4),
                        rhs_scale=scales[i][:, g, :],
                        start=(g == 0),
                        stop=(g == PASSES - 1),
                    )
            for h in range(2):
                w = first_weight(i // PIECES // BATCH) + h
                nc.scalar.activation(
                    out=y_cols[i][:, h, :], in_=acc[:, h, :], func=ACT.Identity, bias=bias_col[:, w : w + 1], scale=1.0
                )

        def turn_back(i):
            sum_sq[i] = work.tile([P, 2, PIECE_BLOCKS], F32, name="sum_sq")
            squares = work.tile([P, 2, PIECE_BLOCKS, D], F32, name="squares")
            y = back_pool.tile([P, 2, PIECE_BLOCKS, D], F32, tag="back", name="back")
            ys[i] = y
            for h in range(2):
                for j in range(PIECE_BLOCKS):
                    nc.tensor.transpose(
                        out=y[:, h, j, :], in_=y_cols[i][:, h, j * P : (j + 1) * P], identity=ident[:]
                    )
            for h in range(2):
                for j in range(PIECE_BLOCKS):
                    nc.scalar.activation(
                        out=squares[:, h, j, :], in_=y[:, h, j, :], func=ACT.Square, accum_out=sum_sq[i][:, h, j : j + 1]
                    )

        def norm(i):
            inv_rms[i] = work.tile([P, 2, PIECE_BLOCKS], F32, name="inv_rms")
            nc.scalar.activation(
                out=inv_rms[i][:].rearrange("p h j -> p (h j)"), in_=sum_sq[i][:].rearrange("p h j -> p (h j)"),
                func=ACT.Abs_reciprocal_sqrt, bias=eps[:, 0:1], scale=1.0 / D,
            )

        def rotate_store(i):
            c, half = divmod(i, PIECES)
            s, b = divmod(c, BATCH)
            products = product_pool.tile([P, 2, PIECE_BLOCKS, 2, D], F32, name="products")
            if half == 0:
                result[c] = out_pool.tile([P, PIECES, 2, PIECE_BLOCKS, D], F32, name="result")
            last = i == N_PIECES - 1

            def add(engine, heads):
                flat = products[:, heads].rearrange("p h j k d -> p (h j) k d")
                engine.tensor_tensor(
                    out=pairs(result[c][:, half, heads].rearrange("p h j d -> p (h j) d")),
                    in0=pairs(flat[:, :, 0, :]), in1=pairs(flat[:, :, 1, :])[:, :, :, ::-1], op=ALU.add,
                )

            for h in range(2):
                for j in range(PIECE_BLOCKS):
                    nc.vector.scalar_tensor_tensor(
                        out=products[:, h, j], in0=ys[i][:, h, j, :].unsqueeze(1).to_broadcast([P, 2, D]),
                        scalar=inv_rms[i][:, h, j : j + 1], in1=tables[:, s, h, PIECE_BLOCKS * half + j],
                        op0=ALU.mult, op1=ALU.mult,
                    )
                if last:
                    add(nc.gpsimd if h == 0 else nc.vector, slice(h, h + 1))
            if not last:
                add(nc.gpsimd, slice(0, 2))
            stored = slice(half, half + 1) if c == N_CHUNKS - 1 else slice(0, PIECES)
            if stored.stop == half + 1:
                for h in range(2):
                    nc.sync.dma_start(
                        out=outs[h][b, s * CHUNK : (s + 1) * CHUNK, 0, :].rearrange(
                            "(p f j) d -> p f (j d)", f=PIECES, j=PIECE_BLOCKS
                        )[:, stored, :],
                        in_=result[c][:, stored, h].rearrange("p f j d -> p f (j d)"),
                    )

        with tc.manual_schedule():
            for i in range(N_PIECES + BACK_LAG):
                c, half = divmod(i, PIECES)
                now, mid, old = i < N_PIECES, 0 <= i - MX_LAG < N_PIECES, i >= BACK_LAG
                if half == 0:
                    if 1 <= c and c + LOAD_AHEAD < N_CHUNKS:
                        x_tiles[c + LOAD_AHEAD] = load(c + LOAD_AHEAD)
                    if c == 1:
                        load_weight(0)
                        load_weight(1)
                    if c in (2, 3):
                        load_rotary(nc.sync, slice(c, c + 1))
                    if c >= 2 and c - 2 + BATCH < N_CHUNKS:
                        fill_table(nc.gpsimd, (c - 2) // BATCH + 1, (c - 2) % BATCH)
                if old:
                    turn_back(i - BACK_LAG)
                if mid and i > MX_LAG:
                    project(i - MX_LAG)
                if old:
                    norm(i - BACK_LAG)
                if now:
                    open_piece(i)
                    turn(i, 0, nc.scalar.copy)
                if i == 2:
                    spread_biases()
                if now:
                    turn(i, 1, nc.vector.tensor_copy if i % 6 in VECTOR_COPIES else nc.scalar.copy)
                if i == MX_LAG:
                    project(0)
                if i == 3:
                    spread_gains(TEXT)
                    spread_gains(IMAGE)
                if old:
                    rotate_store(i - BACK_LAG)
                if now:
                    quantise(i)
                if 3 <= i < 3 + PIECES:
                    ts = slice(PIECE_BLOCKS * (i - 3), PIECE_BLOCKS * (i - 2))
                    for piece in range(TABLE_PIECES):
                        fill_table(nc.vector, 0, piece, ts)
